import numpy as np
import ml_dtypes


def mxq(x, axis, fmt="e4m3"):
    dtype, down = {"e4m3": (ml_dtypes.float8_e4m3fn, 7), "e5m2": (ml_dtypes.float8_e5m2, 14)}[fmt]
    v = np.moveaxis(np.asarray(x, np.float32).astype(ml_dtypes.bfloat16).astype(np.float64), axis, -1)
    blocks = v.reshape(v.shape[:-1] + (-1, 32))
    amax = np.abs(blocks).max(-1, keepdims=True)
    byte = np.maximum(np.where(amax > 0, np.frexp(amax)[1] - 1 + 127, 0) - down, 1)
    scale = np.exp2(byte - 127.0)
    codes = (blocks / scale).astype(np.float32).astype(dtype).astype(np.float64)
    return np.moveaxis((codes * scale).reshape(v.shape), -1, axis)


WIDE = False


def mx_kscale(k):
    if not WIDE:
        return np.ones(k)
    levels = np.array([10, -10, 5, -5, 0])
    a = np.random.permutation(np.resize(levels, k // 512 * 4)).reshape(k // 512, 4)
    idx = np.arange(k)
    return np.exp2(a[idx // 512, idx % 128 // 32])


BF16 = ml_dtypes.bfloat16


def bf(x):
    return np.asarray(x, np.float32).astype(BF16)


def f64(x):
    return np.asarray(x).astype(np.float64)


B, L, E, H = 4, 1024, 512, 4
HD = E // H
EPS = 1e-12


def l2_normalize(t):
    n = np.sqrt(np.sum(t * t, axis=-1, keepdims=True))
    return t / np.maximum(n, EPS)


def setup_inputs():
    s = mx_kscale(E)
    return {"x": bf(np.random.standard_normal((B, L, E)) * s),
            "W": bf(np.random.standard_normal((3 * E, E)) / np.sqrt(E) / s[None, :]),
            "b": bf(np.random.standard_normal(3 * E) * 0.3)}


def reference(x, W, b):
    y = (mxq(f64(x), 2, "e4m3") @ mxq(f64(W), 1, "e4m3").T) + f64(b)
    y = y.reshape(B, L, H, 3, HD)
    q = np.transpose(y[..., 0, :], (0, 2, 1, 3))
    k = np.transpose(y[..., 1, :], (0, 2, 1, 3))
    v = np.transpose(y[..., 2, :], (0, 2, 1, 3))
    return l2_normalize(q), l2_normalize(k), v

@@ -1,0 +1,331 @@
+from contextlib import ExitStack
+
+import concourse.mybir as mybir
+from concourse.masks import make_identity
+
+FP8X4 = mybir.dt.float8_e4m3fn_x4
+F32 = mybir.dt.float32
+BF16 = mybir.dt.bfloat16
+U32 = mybir.dt.uint32
+U8 = mybir.dt.uint8
+ACT = mybir.ActivationFunctionType
+ALU = mybir.AluOpType
+
+B, L, E, H = 4, 1024, 512, 4
+HD = E // H
+P = 128
+T = L // P
+NT = B * T
+EPS = 1e-12
+FLOPS = 2 * B * L * E * 3 * E
+
+CHAINS = [(i, 2) for i in range(0, 32, 2)]
+STORES_QK = [(i, 4) for i in range(0, 28, 4)] + [(28, 2), (30, 2)]
+STORES_V = [(i, 4) for i in range(0, 28, 4)] + [(28, 2), (30, 2)]
+FAST = 3
+GV = 2
+DG = 3.6
+DVF = 1.5
+GV_EARLY = []
+LOAD_KEY = [None, None, None, None]
+DX, DE, DQ = 12.0, 11.0, 5.0
+LS = 1.1
+DV = 6.5
+DSQ, DSK = 8.0, 12.0
+E_ENG = "ss"
+TAIL_V = 0
+S_ORDER = (0, 2, 1)
+REST = "v"
+LATE = 5.0
+
+
+def tile_selfattention_pa_t_kernel(tc, x, W, b, out_0, out_1, out_2):
+    nc = tc.nc
+    outs = (out_0, out_1, out_2)
+    with ExitStack() as ctx:
+        ctx.enter_context(tc.manual_schedule())
+        const = ctx.enter_context(tc.tile_pool(name="const", bufs=1))
+        grp = ctx.enter_context(tc.tile_pool(name="grp", bufs=6))
+        cod = ctx.enter_context(tc.tile_pool(name="cod", bufs=6))
+        stg = ctx.enter_context(tc.tile_pool(name="stg", bufs=3))
+        small = ctx.enter_context(tc.tile_pool(name="small", bufs=6))
+        ps_t = ctx.enter_context(tc.psum_pool(name="ps_t", bufs=2))
+        ps_a = ctx.enter_context(tc.psum_pool(name="ps_a", bufs=6))
+
+        w_sb = const.tile([P, 3, H, E], BF16)
+        x_sb = const.tile([P, B, T, E], BF16)
+        b_row = const.tile([P, 3 * E], BF16)
+        bias = const.tile([P, 3 * E], BF16)
+        ones = const.tile([P, P], BF16)
+        ident = const.tile([P, P], F32)
+        c_pos = const.tile([P, 1], F32)
+        c_neg = const.tile([P, 1], F32)
+        warm = const.tile([P, 1], F32)
+        junk = const.tile([P, HD], BF16)
+        w_codes = const.tile([P, 3, E], U32, align_bytes=64)
+        w_scales = const.tile([P, 3, E], U8, align_bytes=64)
+        w_view = W.rearrange("(h s p) k -> s p h k", h=H, s=3)
+        bias_v = bias[:].rearrange("p (s h d) -> p s h d", h=H, s=3)
+
+        def load_x(bi, t0, t1):
+            nc.sync.dma_start(
+                out=x_sb[:, bi, t0:t1, :],
+                in_=x[bi].rearrange("(p t) k -> p t k", t=T)[:, t0:t1, :],
+            )
+
+        def load_w(s, h0, h1):
+            nc.sync.dma_start(out=w_sb[:, s, h0:h1, :], in_=w_view[s][:, h0:h1, :])
+
+        nc.vector.memset(b_row[:], 0.0)
+        nc.scalar.dma_start(
+            out=b_row[0:1, :].rearrange("o (s h d) -> o s h d", s=3, h=H),
+            in_=b.rearrange("(o h s d) -> o s h d", o=1, h=H, s=3),
+        )
+        load_x(0, 0, 2)
+        load_w(S_ORDER[0], 0, 2)
+        load_w(S_ORDER[0], 2, 4)
+        load_x(0, 2, 4)
+        load_w(S_ORDER[1], 0, 4)
+        load_w(S_ORDER[2], 0, 4)
+        load_x(0, 4, T)
+        for bi in range(1, B):
+            if LOAD_KEY[bi] is None:
+                load_x(bi, 0, T)
+
+        make_identity(nc, ident[:])
+        nc.vector.memset(ones[:], 1.0)
+        nc.vector.memset(c_pos[:], EPS * EPS)
+        nc.vector.memset(c_neg[:], -EPS * EPS)
+        nc.scalar.activation(out=warm[:], in_=c_pos[:], func=ACT.Abs_reciprocal_sqrt)
+
+        def transposes(rows, pool, name):
+            pt = pool.tile([P, E], F32, name=name)
+            ptv = pt[:].rearrange("p (a r) -> p a r", a=4)
+            for i in range(2):
+                words = rows[i].bitcast(F32)
+                for u in range(2):
+                    nc.tensor.transpose(ptv[:, 2 * i + u, :], words[:, u * P:(u + 1) * P], ident[:])
+            return pt
+
+        def copy_out(bank, engine):
+            g = grp.tile([P, 2 * E], BF16, name="g", align_bytes=64)
+            dst = g[:].bitcast(F32).rearrange("p (i r u) -> p i r u", i=2, u=2)
+            src = bank[:].rearrange("p (i u r) -> p i r u", i=2, u=2)
+            if engine == "v":
+                nc.vector.tensor_copy(out=dst, in_=src)
+            else:
+                nc.scalar.copy(out=dst, in_=src)
+            return g
+
+        def quantise(g, codes, scales):
+            nc.vector.quantize_mx(out=codes.bitcast(FP8X4), scales=scales, in_=g[:])
+
+        wb = {}
+        wg = {}
+
+        def w_transposes(s, a):
+            wb[(s, a)] = transposes([w_sb[:, s, 2 * a + i, :] for i in range(2)], ps_a, "acc")
+
+        def w_copy(s, a, engine):
+            wg[(s, a)] = copy_out(wb[(s, a)], engine)
+
+        def w_quantise(s, a):
+            cols = slice(a * 2 * P, (a + 1) * 2 * P)
+            quantise(wg[(s, a)], w_codes[:, s, cols], w_scales[:, s, cols])
+
+        xb = {}
+        xg = {}
+        xq = {}
+
+        def x_transposes(pi):
+            xb[pi] = transposes([x_sb[:, (2 * pi + j) // T, (2 * pi + j) % T, :] for j in range(2)], ps_t, "pt")
+
+        def x_copy(pi, engine):
+            xg[pi] = copy_out(xb[pi], engine)
+
+        def x_quantise(pi):
+            xc = cod.tile([P, 2 * P], U32, name="xc", align_bytes=64)
+            xs = cod.tile([P, 2 * P], U8, name="xs", align_bytes=64)
+            quantise(xg[pi], xc[:], xs[:])
+            xq[pi] = (xc, xs)
+
+        st = {}
+        accs = {}
+        chain_of = {}
+        for ci, (i0, n) in enumerate(CHAINS):
+            for i in range(i0, i0 + n):
+                chain_of[i] = ci
+        ss = {}
+        rr = {}
+
+        def mx(i, s):
+            xc, xs = xq[i // 2]
+            cols = slice((i % 2) * P, (i % 2 + 1) * P)
+            acc = ps_a.tile([P, E], F32, name="acc")
+            nc.tensor.matmul_mx(
+                out=acc[:],
+                lhsT=xc[:, cols].bitcast(FP8X4), lhsT_scale=xs[:, cols],
+                rhs=w_codes[:, s, :].bitcast(FP8X4), rhs_scale=w_scales[:, s, :],
+                start=True, stop=True,
+            )
+            accs[(i, s)] = acc
+
+        def add_bias(i, s):
+            bi, t = i // T, i % T
+            if bi not in st:
+                st_qk = stg.tile([P, 2, H, T, HD], F32, name="st_qk")
+                st_v = stg.tile([P, H, T, HD], F32, name="st_v")
+                st[bi] = (st_qk[:, 0], st_qk[:, 1], st_v[:], st_qk[:].rearrange("p s h t d -> p (s h) t d"))
+            nc.vector.tensor_tensor(
+                out=st[bi][s][:, :, t, :],
+                in0=accs[(i, s)][:].rearrange("p (h d) -> p h d", h=H),
+                in1=bias_v[:, s], op=ALU.add,
+            )
+
+        def squares(i, s):
+            bi, t = i // T, i % T
+            ci = chain_of[i]
+            i0, n = CHAINS[ci]
+            if ci not in ss:
+                ss_t = small.tile([P, 2, H, n], F32, name="ss")
+                ss[ci] = ss_t
+            for h in range(H):
+                nc.scalar.activation(
+                    out=junk[:], in_=st[bi][s][:, h, t, :], func=ACT.Square,
+                    accum_out=ss[ci][:, s, h, i - i0:i - i0 + 1],
+                )
+
+        def chain_norm(ci):
+            n = CHAINS[ci][1]
+            u = small.tile([P, 2 * H * n], F32, name="u")
+            r = small.tile([P, 2, H, n], F32, name="r")
+            flat = ss[ci][:].rearrange("p s h t -> p (s h t)")
+            nc.scalar.activation(out=u[:], in_=flat, func=ACT.Relu, bias=c_neg[:])
+            nc.scalar.activation(out=r[:].rearrange("p s h t -> p (s h t)"), in_=u[:], func=ACT.Abs_reciprocal_sqrt, bias=c_pos[:])
+            rr[ci] = r
+
+        def scale_g(ci, g0, g1):
+            i0, n = CHAINS[ci]
+            bi, t0 = i0 // T, i0 % T
+            view = st[bi][3][:, g0:g1, t0:t0 + n, :]
+            nc.gpsimd.tensor_tensor(
+                out=view, in0=view,
+                in1=rr[ci][:].rearrange("p s h t -> p (s h) t")[:, g0:g1, :].unsqueeze(3).to_broadcast([P, g1 - g0, n, HD]),
+                op=ALU.mult,
+            )
+
+        def scale_v(ci, s, h):
+            i0, n = CHAINS[ci]
+            bi, t0 = i0 // T, i0 % T
+            for j in range(n):
+                v = st[bi][s][:, h, t0 + j, :]
+                nc.vector.tensor_scalar_mul(out=v, in0=v, scalar1=rr[ci][:, s, h, j:j + 1])
+
+        def scale_s(ci, s, h):
+            i0, n = CHAINS[ci]
+            bi, t0 = i0 // T, i0 % T
+            for j in range(n):
+                v = st[bi][s][:, h, t0 + j, :]
+                nc.scalar.activation(out=v, in_=v, func=ACT.Copy, scale=rr[ci][:, s, h, j:j + 1])
+
+        def store(i0, n, s):
+            bi, t0 = i0 // T, i0 % T
+            nc.sync.dma_start(
+                out=outs[s][bi].rearrange("h (p t) d -> p h t d", t=T)[:, :, t0:t0 + n, :],
+                in_=st[bi][s][:, :, t0:t0 + n, :],
+            )
+
+        seq = [(i, s) for s in S_ORDER for i in range(4)]
+        for i in range(4, NT - TAIL_V):
+            for s in range(3):
+                seq.append((i, s))
+        for i in range(NT - TAIL_V, NT):
+            seq.append((i, 0))
+            seq.append((i, 1))
+        for i in range(NT - TAIL_V, NT):
+            seq.append((i, 2))
+        pos = {}
+        for p, key in enumerate(seq):
+            pos[key] = p
+
+        ops = []
+
+        def op(key, fn, *args):
+            ops.append((key, len(ops), fn, args))
+
+        def bias_matmul(s):
+            pb = ps_a.tile([P, E], F32, name="acc")
+            nc.tensor.matmul(out=pb[:], lhsT=ones[:], rhs=b_row[:, s * E:(s + 1) * E], start=True, stop=True)
+            accs[("b", s)] = pb
+
+        def bias_copy(s, engine):
+            if engine == "s":
+                nc.scalar.copy(out=bias[:, s * E:(s + 1) * E], in_=accs[("b", s)][:])
+            else:
+                nc.vector.tensor_copy(out=bias[:, s * E:(s + 1) * E], in_=accs[("b", s)][:])
+
+        for bi in range(1, B):
+            if LOAD_KEY[bi] is not None:
+                op(LOAD_KEY[bi], load_x, bi, 0, T)
+
+        s0, s1, s2 = S_ORDER
+        op(-20.0, bias_matmul, s0)
+        op(-19.99, bias_matmul, s1)
+        op(-19.98, bias_matmul, s2)
+        op(-19.9, bias_copy, s0, "s")
+        op(-19.89, bias_copy, s1, "v")
+        op(-19.88, bias_copy, s2, "s")
+        op(-19.0, x_transposes, 0)
+        op(-18.9, x_copy, 0, "v")
+        op(-18.5, x_quantise, 0)
+        op(-18.0, w_transposes, s0, 0)
+        op(-17.9, w_copy, s0, 0, "s")
+        op(-17.0, w_transposes, s0, 1)
+        op(-16.9, w_copy, s0, 1, "v")
+        op(-16.8, w_quantise, s0, 0)
+        op(-16.7, w_quantise, s0, 1)
+        op(-16.0, x_transposes, 1)
+        op(-15.9, x_copy, 1, "s")
+        op(-15.5, x_quantise, 1)
+        for s in (s1, s2):
+            k0 = -0.1 if s == s1 else 2.45
+            for a in range(2):
+                op(k0 + 0.01 * a, w_transposes, s, a)
+                op(k0 + 0.03 + 0.01 * a, w_copy, s, a, "s")
+                op((1.5 if s == s1 else 3.5) + 0.01 * a, w_quantise, s, a)
+
+        for p, (i, s) in enumerate(seq):
+            op(p - 0.6, mx, i, s)
+            op(p, add_bias, i, s)
+            if s < 2:
+                op(p + LS, squares, i, s)
+        for pi in range(2, NT // 2):
+            first = pos[((pi // 2) * 4, 0)]
+            late = LATE if pi < 4 else 0.0
+            op(first - DX + late + 0.01 * pi, x_transposes, pi)
+            op(first - DE + late + 0.01 * pi, x_copy, pi, E_ENG[pi % len(E_ENG)])
+            op(first - DQ + 0.01 * pi, x_quantise, pi)
+        done = {}
+        for ci, (i0, n) in enumerate(CHAINS):
+            e = pos[(i0 + n - 1, 1)]
+            op(e + LS + 0.01, chain_norm, ci)
+            gv = GV if ci < len(CHAINS) - FAST else 8
+            if ci < len(GV_EARLY):
+                gv = GV_EARLY[ci]
+            if gv < 8:
+                op(e + LS + 0.02, scale_g, ci, gv, 8)
+            for g in range(gv):
+                if ci >= len(CHAINS) - FAST and g % 3 == 2:
+                    op(e + LS + 0.03, scale_s, ci, g // H, g % H)
+                else:
+                    op(e + (DV if gv < 8 else DVF) + 0.01 * g, scale_v, ci, g // H, g % H)
+            for i in range(i0, i0 + n):
+                done[i] = e + (DG * n if gv < 8 else DVF + 0.2)
+        for i0, n in STORES_QK:
+            for s in range(2):
+                op(done[i0 + n - 1] + 0.01 * s, store, i0, n, s)
+        for i0, n in STORES_V:
+            op(pos[(i0 + n - 1, 2)] + 0.3, store, i0, n, 2)
+
+        for key, n, fn, args in sorted(ops, key=lambda o: (o[0], o[1])):
+            fn(*args)

@@ -19,24 +19,11 @@ NT = B * T
 EPS = 1e-12
 FLOPS = 2 * B * L * E * 3 * E
 
-CHAINS = [(i, 2) for i in range(0, 32, 2)]
-STORES_QK = [(i, 4) for i in range(0, 28, 4)] + [(28, 2), (30, 2)]
-STORES_V = [(i, 4) for i in range(0, 28, 4)] + [(28, 2), (30, 2)]
-FAST = 3
-GV = 2
-DG = 3.6
-DVF = 1.5
-GV_EARLY = []
-LOAD_KEY = [None, None, None, None]
-DX, DE, DQ = 12.0, 11.0, 5.0
-LS = 1.1
-DV = 6.5
-DSQ, DSK = 8.0, 12.0
-E_ENG = "ss"
-TAIL_V = 0
-S_ORDER = (0, 2, 1)
-REST = "v"
-LATE = 5.0
+FIRST = 4
+AHEAD = 2
+V_GROUPS = 6
+V_LAG = 2
+BLOCKS = [4, 4, 4, 4, 4, 4, 4, 2, 1, 1]
 
 
 def tile_selfattention_pa_t_kernel(tc, x, W, b, out_0, out_1, out_2):
@@ -45,8 +32,8 @@ def tile_selfattention_pa_t_kernel(tc, x, W, b, out_0, out_1, out_2):
     with ExitStack() as ctx:
         ctx.enter_context(tc.manual_schedule())
         const = ctx.enter_context(tc.tile_pool(name="const", bufs=1))
-        grp = ctx.enter_context(tc.tile_pool(name="grp", bufs=6))
-        cod = ctx.enter_context(tc.tile_pool(name="cod", bufs=6))
+        grp = ctx.enter_context(tc.tile_pool(name="grp", bufs=4))
+        cod = ctx.enter_context(tc.tile_pool(name="cod", bufs=5))
         stg = ctx.enter_context(tc.tile_pool(name="stg", bufs=3))
         small = ctx.enter_context(tc.tile_pool(name="small", bufs=6))
         ps_t = ctx.enter_context(tc.psum_pool(name="ps_t", bufs=2))
@@ -55,7 +42,7 @@ def tile_selfattention_pa_t_kernel(tc, x, W, b, out_0, out_1, out_2):
         w_sb = const.tile([P, 3, H, E], BF16)
         x_sb = const.tile([P, B, T, E], BF16)
         b_row = const.tile([P, 3 * E], BF16)
-        bias = const.tile([P, 3 * E], BF16)
+        bias = const.tile([P, 3, H, HD], BF16)
         ones = const.tile([P, P], BF16)
         ident = const.tile([P, P], F32)
         c_pos = const.tile([P, 1], F32)
@@ -65,7 +52,6 @@ def tile_selfattention_pa_t_kernel(tc, x, W, b, out_0, out_1, out_2):
         w_codes = const.tile([P, 3, E], U32, align_bytes=64)
         w_scales = const.tile([P, 3, E], U8, align_bytes=64)
         w_view = W.rearrange("(h s p) k -> s p h k", h=H, s=3)
-        bias_v = bias[:].rearrange("p (s h d) -> p s h d", h=H, s=3)
 
         def load_x(bi, t0, t1):
             nc.sync.dma_start(
@@ -73,24 +59,20 @@ def tile_selfattention_pa_t_kernel(tc, x, W, b, out_0, out_1, out_2):
                 in_=x[bi].rearrange("(p t) k -> p t k", t=T)[:, t0:t1, :],
             )
 
-        def load_w(s, h0, h1):
-            nc.sync.dma_start(out=w_sb[:, s, h0:h1, :], in_=w_view[s][:, h0:h1, :])
-
         nc.vector.memset(b_row[:], 0.0)
         nc.scalar.dma_start(
             out=b_row[0:1, :].rearrange("o (s h d) -> o s h d", s=3, h=H),
             in_=b.rearrange("(o h s d) -> o s h d", o=1, h=H, s=3),
         )
         load_x(0, 0, 2)
-        load_w(S_ORDER[0], 0, 2)
-        load_w(S_ORDER[0], 2, 4)
+        nc.sync.dma_start(out=w_sb[:, 0, 0:2, :], in_=w_view[0][:, 0:2, :])
+        nc.sync.dma_start(out=w_sb[:, 0, 2:4, :], in_=w_view[0][:, 2:4, :])
         load_x(0, 2, 4)
-        load_w(S_ORDER[1], 0, 4)
-        load_w(S_ORDER[2], 0, 4)
+        nc.sync.dma_start(out=w_sb[:, 1], in_=w_view[1])
+        nc.sync.dma_start(out=w_sb[:, 2], in_=w_view[2])
         load_x(0, 4, T)
         for bi in range(1, B):
-            if LOAD_KEY[bi] is None:
-                load_x(bi, 0, T)
+            load_x(bi, 0, T)
 
         make_identity(nc, ident[:])
         nc.vector.memset(ones[:], 1.0)
@@ -99,18 +81,17 @@ def tile_selfattention_pa_t_kernel(tc, x, W, b, out_0, out_1, out_2):
         nc.scalar.activation(out=warm[:], in_=c_pos[:], func=ACT.Abs_reciprocal_sqrt)
 
         def transposes(rows, pool, name):
-            pt = pool.tile([P, E], F32, name=name)
-            ptv = pt[:].rearrange("p (a r) -> p a r", a=4)
+            bank = pool.tile([P, 2, 2, P], F32, name=name)
             for i in range(2):
                 words = rows[i].bitcast(F32)
                 for u in range(2):
-                    nc.tensor.transpose(ptv[:, 2 * i + u, :], words[:, u * P:(u + 1) * P], ident[:])
-            return pt
+                    nc.tensor.transpose(bank[:, i, u, :], words[:, u * P:(u + 1) * P], ident[:])
+            return bank
 
         def copy_out(bank, engine):
             g = grp.tile([P, 2 * E], BF16, name="g", align_bytes=64)
             dst = g[:].bitcast(F32).rearrange("p (i r u) -> p i r u", i=2, u=2)
-            src = bank[:].rearrange("p (i u r) -> p i r u", i=2, u=2)
+            src = bank[:].rearrange("p i u r -> p i r u")
             if engine == "v":
                 nc.vector.tensor_copy(out=dst, in_=src)
             else:
@@ -120,212 +101,146 @@ def tile_selfattention_pa_t_kernel(tc, x, W, b, out_0, out_1, out_2):
         def quantise(g, codes, scales):
             nc.vector.quantize_mx(out=codes.bitcast(FP8X4), scales=scales, in_=g[:])
 
-        wb = {}
-        wg = {}
+        def w_grouped(s, engines):
+            banks = [transposes([w_sb[:, s, 2 * a + i, :] for i in range(2)], ps_a, "acc") for a in range(2)]
+            return [copy_out(banks[a], engines[a]) for a in range(2)]
 
-        def w_transposes(s, a):
-            wb[(s, a)] = transposes([w_sb[:, s, 2 * a + i, :] for i in range(2)], ps_a, "acc")
+        def w_quantise(s, gs):
+            for a in range(2):
+                cols = slice(a * 2 * P, (a + 1) * 2 * P)
+                quantise(gs[a], w_codes[:, s, cols], w_scales[:, s, cols])
 
-        def w_copy(s, a, engine):
-            wg[(s, a)] = copy_out(wb[(s, a)], engine)
+        def x_grouped(pi, engine):
+            rows = [x_sb[:, (2 * pi + j) // T, (2 * pi + j) % T, :] for j in range(2)]
+            return copy_out(transposes(rows, ps_t, "pt"), engine)
 
-        def w_quantise(s, a):
-            cols = slice(a * 2 * P, (a + 1) * 2 * P)
-            quantise(wg[(s, a)], w_codes[:, s, cols], w_scales[:, s, cols])
+        x_mx = {}
 
-        xb = {}
-        xg = {}
-        xq = {}
-
-        def x_transposes(pi):
-            xb[pi] = transposes([x_sb[:, (2 * pi + j) // T, (2 * pi + j) % T, :] for j in range(2)], ps_t, "pt")
-
-        def x_copy(pi, engine):
-            xg[pi] = copy_out(xb[pi], engine)
-
-        def x_quantise(pi):
+        def x_quantise(pi, g):
             xc = cod.tile([P, 2 * P], U32, name="xc", align_bytes=64)
             xs = cod.tile([P, 2 * P], U8, name="xs", align_bytes=64)
-            quantise(xg[pi], xc[:], xs[:])
-            xq[pi] = (xc, xs)
+            quantise(g, xc[:], xs[:])
+            x_mx[pi] = (xc, xs)
 
-        st = {}
-        accs = {}
-        chain_of = {}
-        for ci, (i0, n) in enumerate(CHAINS):
-            for i in range(i0, i0 + n):
-                chain_of[i] = ci
-        ss = {}
-        rr = {}
+        stage = {}
+        sumsq = {}
+        rnorm = {}
 
-        def mx(i, s):
-            xc, xs = xq[i // 2]
+        def target(i, s):
+            st_qk, st_v = stage[i // T]
+            if s == 2:
+                return st_v[:, :, i % T, :]
+            return st_qk[:, s, :, i % T, :]
+
+        def one_pass(i, s):
+            if i // T not in stage:
+                st_qk = stg.tile([P, 2, H, T, HD], F32, name="st_qk")
+                st_v = stg.tile([P, H, T, HD], F32, name="st_v")
+                stage[i // T] = (st_qk, st_v)
+            xc, xs = x_mx[i // 2]
             cols = slice((i % 2) * P, (i % 2 + 1) * P)
-            acc = ps_a.tile([P, E], F32, name="acc")
+            acc = ps_a.tile([P, H, HD], F32, name="acc")
             nc.tensor.matmul_mx(
-                out=acc[:],
+                out=acc[:].rearrange("p h d -> p (h d)"),
                 lhsT=xc[:, cols].bitcast(FP8X4), lhsT_scale=xs[:, cols],
                 rhs=w_codes[:, s, :].bitcast(FP8X4), rhs_scale=w_scales[:, s, :],
                 start=True, stop=True,
             )
-            accs[(i, s)] = acc
-
-        def add_bias(i, s):
-            bi, t = i // T, i % T
-            if bi not in st:
-                st_qk = stg.tile([P, 2, H, T, HD], F32, name="st_qk")
-                st_v = stg.tile([P, H, T, HD], F32, name="st_v")
-                st[bi] = (st_qk[:, 0], st_qk[:, 1], st_v[:], st_qk[:].rearrange("p s h t d -> p (s h) t d"))
-            nc.vector.tensor_tensor(
-                out=st[bi][s][:, :, t, :],
-                in0=accs[(i, s)][:].rearrange("p (h d) -> p h d", h=H),
-                in1=bias_v[:, s], op=ALU.add,
-            )
-
-        def squares(i, s):
-            bi, t = i // T, i % T
-            ci = chain_of[i]
-            i0, n = CHAINS[ci]
-            if ci not in ss:
-                ss_t = small.tile([P, 2, H, n], F32, name="ss")
-                ss[ci] = ss_t
+            nc.vector.tensor_tensor(out=target(i, s), in0=acc[:], in1=bias[:, s], op=ALU.add)
+            if s == 2:
+                return
+            if i not in sumsq:
+                ss = small.tile([P, 2, H], F32, name="ss")
+                sumsq[i] = ss
             for h in range(H):
                 nc.scalar.activation(
-                    out=junk[:], in_=st[bi][s][:, h, t, :], func=ACT.Square,
-                    accum_out=ss[ci][:, s, h, i - i0:i - i0 + 1],
+                    out=junk[:], in_=target(i, s)[:, h, :], func=ACT.Square, accum_out=sumsq[i][:, s, h:h + 1]
                 )
 
-        def chain_norm(ci):
-            n = CHAINS[ci][1]
-            u = small.tile([P, 2 * H * n], F32, name="u")
-            r = small.tile([P, 2, H, n], F32, name="r")
-            flat = ss[ci][:].rearrange("p s h t -> p (s h t)")
-            nc.scalar.activation(out=u[:], in_=flat, func=ACT.Relu, bias=c_neg[:])
-            nc.scalar.activation(out=r[:].rearrange("p s h t -> p (s h t)"), in_=u[:], func=ACT.Abs_reciprocal_sqrt, bias=c_pos[:])
-            rr[ci] = r
-
-        def scale_g(ci, g0, g1):
-            i0, n = CHAINS[ci]
-            bi, t0 = i0 // T, i0 % T
-            view = st[bi][3][:, g0:g1, t0:t0 + n, :]
-            nc.gpsimd.tensor_tensor(
-                out=view, in0=view,
-                in1=rr[ci][:].rearrange("p s h t -> p (s h) t")[:, g0:g1, :].unsqueeze(3).to_broadcast([P, g1 - g0, n, HD]),
-                op=ALU.mult,
+        def norms(i):
+            u = small.tile([P, 2 * H], F32, name="u")
+            r = small.tile([P, 2, H], F32, name="r")
+            nc.scalar.activation(out=u[:], in_=sumsq[i][:].rearrange("p s h -> p (s h)"), func=ACT.Relu, bias=c_neg[:])
+            nc.scalar.activation(
+                out=r[:].rearrange("p s h -> p (s h)"), in_=u[:], func=ACT.Abs_reciprocal_sqrt, bias=c_pos[:]
             )
+            rnorm[i] = r
 
-        def scale_v(ci, s, h):
-            i0, n = CHAINS[ci]
-            bi, t0 = i0 // T, i0 % T
-            for j in range(n):
-                v = st[bi][s][:, h, t0 + j, :]
-                nc.vector.tensor_scalar_mul(out=v, in0=v, scalar1=rr[ci][:, s, h, j:j + 1])
+        def scale_on_scalar(i):
+            for g in range(V_GROUPS, 2 * H):
+                view = target(i, g // H)[:, g % H, :]
+                nc.scalar.activation(out=view, in_=view, func=ACT.Copy, scale=rnorm[i][:, g // H, g % H:g % H + 1])
 
-        def scale_s(ci, s, h):
-            i0, n = CHAINS[ci]
-            bi, t0 = i0 // T, i0 % T
-            for j in range(n):
-                v = st[bi][s][:, h, t0 + j, :]
-                nc.scalar.activation(out=v, in_=v, func=ACT.Copy, scale=rr[ci][:, s, h, j:j + 1])
+        def scale_on_vector(i):
+            for g in range(V_GROUPS):
+                view = target(i, g // H)[:, g % H, :]
+                nc.vector.tensor_scalar_mul(out=view, in0=view, scalar1=rnorm[i][:, g // H, g % H:g % H + 1])
 
-        def store(i0, n, s):
-            bi, t0 = i0 // T, i0 % T
-            nc.sync.dma_start(
-                out=outs[s][bi].rearrange("h (p t) d -> p h t d", t=T)[:, :, t0:t0 + n, :],
-                in_=st[bi][s][:, :, t0:t0 + n, :],
+        block_end = {}
+        i0 = 0
+        for n in BLOCKS:
+            block_end[i0 + n - 1] = n
+            i0 += n
+
+        def store(i, s_list):
+            if i not in block_end:
+                return
+            n = block_end[i]
+            bi, t0 = i // T, i % T - n + 1
+            st_qk, st_v = stage[bi]
+            for s in s_list:
+                src = st_v[:, :, t0:t0 + n, :] if s == 2 else st_qk[:, s, :, t0:t0 + n, :]
+                nc.sync.dma_start(
+                    out=outs[s][bi].rearrange("h (p t) d -> p h t d", t=T)[:, :, t0:t0 + n, :], in_=src
+                )
+
+        for s in range(3):
+            pb = ps_a.tile([P, H, HD], F32, name="acc")
+            nc.tensor.matmul(
+                out=pb[:].rearrange("p h d -> p (h d)"), lhsT=ones[:], rhs=b_row[:, s * E:(s + 1) * E],
+                start=True, stop=True,
             )
-
-        seq = [(i, s) for s in S_ORDER for i in range(4)]
-        for i in range(4, NT - TAIL_V):
-            for s in range(3):
-                seq.append((i, s))
-        for i in range(NT - TAIL_V, NT):
-            seq.append((i, 0))
-            seq.append((i, 1))
-        for i in range(NT - TAIL_V, NT):
-            seq.append((i, 2))
-        pos = {}
-        for p, key in enumerate(seq):
-            pos[key] = p
-
-        ops = []
-
-        def op(key, fn, *args):
-            ops.append((key, len(ops), fn, args))
-
-        def bias_matmul(s):
-            pb = ps_a.tile([P, E], F32, name="acc")
-            nc.tensor.matmul(out=pb[:], lhsT=ones[:], rhs=b_row[:, s * E:(s + 1) * E], start=True, stop=True)
-            accs[("b", s)] = pb
-
-        def bias_copy(s, engine):
-            if engine == "s":
-                nc.scalar.copy(out=bias[:, s * E:(s + 1) * E], in_=accs[("b", s)][:])
+            if s == 1:
+                nc.vector.tensor_copy(out=bias[:, s], in_=pb[:])
             else:
-                nc.vector.tensor_copy(out=bias[:, s * E:(s + 1) * E], in_=accs[("b", s)][:])
+                nc.scalar.copy(out=bias[:, s], in_=pb[:])
 
-        for bi in range(1, B):
-            if LOAD_KEY[bi] is not None:
-                op(LOAD_KEY[bi], load_x, bi, 0, T)
-
-        s0, s1, s2 = S_ORDER
-        op(-20.0, bias_matmul, s0)
-        op(-19.99, bias_matmul, s1)
-        op(-19.98, bias_matmul, s2)
-        op(-19.9, bias_copy, s0, "s")
-        op(-19.89, bias_copy, s1, "v")
-        op(-19.88, bias_copy, s2, "s")
-        op(-19.0, x_transposes, 0)
-        op(-18.9, x_copy, 0, "v")
-        op(-18.5, x_quantise, 0)
-        op(-18.0, w_transposes, s0, 0)
-        op(-17.9, w_copy, s0, 0, "s")
-        op(-17.0, w_transposes, s0, 1)
-        op(-16.9, w_copy, s0, 1, "v")
-        op(-16.8, w_quantise, s0, 0)
-        op(-16.7, w_quantise, s0, 1)
-        op(-16.0, x_transposes, 1)
-        op(-15.9, x_copy, 1, "s")
-        op(-15.5, x_quantise, 1)
-        for s in (s1, s2):
-            k0 = -0.1 if s == s1 else 2.45
-            for a in range(2):
-                op(k0 + 0.01 * a, w_transposes, s, a)
-                op(k0 + 0.03 + 0.01 * a, w_copy, s, a, "s")
-                op((1.5 if s == s1 else 3.5) + 0.01 * a, w_quantise, s, a)
-
-        for p, (i, s) in enumerate(seq):
-            op(p - 0.6, mx, i, s)
-            op(p, add_bias, i, s)
+        gx = {0: x_grouped(0, "v")}
+        gw = w_grouped(0, "sv")
+        x_quantise(0, gx[0])
+        gx[1] = x_grouped(1, "s")
+        for s in range(3):
+            w_quantise(s, gw)
+            if s == 0:
+                x_quantise(1, gx[1])
             if s < 2:
-                op(p + LS, squares, i, s)
-        for pi in range(2, NT // 2):
-            first = pos[((pi // 2) * 4, 0)]
-            late = LATE if pi < 4 else 0.0
-            op(first - DX + late + 0.01 * pi, x_transposes, pi)
-            op(first - DE + late + 0.01 * pi, x_copy, pi, E_ENG[pi % len(E_ENG)])
-            op(first - DQ + 0.01 * pi, x_quantise, pi)
-        done = {}
-        for ci, (i0, n) in enumerate(CHAINS):
-            e = pos[(i0 + n - 1, 1)]
-            op(e + LS + 0.01, chain_norm, ci)
-            gv = GV if ci < len(CHAINS) - FAST else 8
-            if ci < len(GV_EARLY):
-                gv = GV_EARLY[ci]
-            if gv < 8:
-                op(e + LS + 0.02, scale_g, ci, gv, 8)
-            for g in range(gv):
-                if ci >= len(CHAINS) - FAST and g % 3 == 2:
-                    op(e + LS + 0.03, scale_s, ci, g // H, g % H)
-                else:
-                    op(e + (DV if gv < 8 else DVF) + 0.01 * g, scale_v, ci, g // H, g % H)
-            for i in range(i0, i0 + n):
-                done[i] = e + (DG * n if gv < 8 else DVF + 0.2)
-        for i0, n in STORES_QK:
-            for s in range(2):
-                op(done[i0 + n - 1] + 0.01 * s, store, i0, n, s)
-        for i0, n in STORES_V:
-            op(pos[(i0 + n - 1, 2)] + 0.3, store, i0, n, 2)
+                gw = w_grouped(s + 1, "ss")
+            else:
+                for pi in range(FIRST // 2, FIRST // 2 + AHEAD):
+                    gx[pi] = x_grouped(pi, "s")
+            for i in range(FIRST):
+                one_pass(i, s)
+                if s == 1:
+                    norms(i)
+                    scale_on_scalar(i)
+                if s == 2:
+                    scale_on_vector(i)
+                    if i % 2 == 1:
+                        x_quantise((FIRST + i) // 2, gx[(FIRST + i) // 2])
+        store(FIRST - 1, (2, 0, 1))
 
-        for key, n, fn, args in sorted(ops, key=lambda o: (o[0], o[1])):
-            fn(*args)
+        for i in range(FIRST, NT + V_LAG):
+            if i < NT:
+                pi = i // 2 + AHEAD
+                if i % 2 == 0 and 2 * pi < NT:
+                    gx[pi] = x_grouped(pi, "s")
+                for s in range(3):
+                    one_pass(i, s)
+                norms(i)
+                scale_on_scalar(i)
+                store(i, (2,))
+                if i % 2 == 1 and 2 * pi < NT:
+                    x_quantise(pi, gx[pi])
+            if i - V_LAG >= FIRST:
+                scale_on_vector(i - V_LAG)
+                store(i - V_LAG, (0, 1))

@@ -21,8 +21,10 @@ FLOPS = 2 * B * L * E * 3 * E
 
 FIRST = 4
 AHEAD = 2
-V_GROUPS = 6
-V_LAG = 2
+V_GROUPS = 2
+S_GROUPS = 0
+LAG = 2
+RING = 8
 BLOCKS = [4, 4, 4, 4, 4, 4, 4, 2, 1, 1]
 
 
@@ -48,7 +50,7 @@ def tile_selfattention_pa_t_kernel(tc, x, W, b, out_0, out_1, out_2):
         c_pos = const.tile([P, 1], F32)
         c_neg = const.tile([P, 1], F32)
         warm = const.tile([P, 1], F32)
-        junk = const.tile([P, HD], BF16)
+        junk = const.tile([P, RING, HD], BF16)
         w_codes = const.tile([P, 3, E], U32, align_bytes=64)
         w_scales = const.tile([P, 3, E], U8, align_bytes=64)
         w_view = W.rearrange("(h s p) k -> s p h k", h=H, s=3)
@@ -154,27 +156,35 @@ def tile_selfattention_pa_t_kernel(tc, x, W, b, out_0, out_1, out_2):
                 sumsq[i] = ss
             for h in range(H):
                 nc.scalar.activation(
-                    out=junk[:], in_=target(i, s)[:, h, :], func=ACT.Square, accum_out=sumsq[i][:, s, h:h + 1]
+                    out=junk[:, (s * H + h) % RING, :], in_=target(i, s)[:, h, :], func=ACT.Square,
+                    accum_out=sumsq[i][:, s, h:h + 1],
                 )
 
-        def norms(i):
+        def clamp(i):
             u = small.tile([P, 2 * H], F32, name="u")
-            r = small.tile([P, 2, H], F32, name="r")
             nc.scalar.activation(out=u[:], in_=sumsq[i][:].rearrange("p s h -> p (s h)"), func=ACT.Relu, bias=c_neg[:])
-            nc.scalar.activation(
-                out=r[:].rearrange("p s h -> p (s h)"), in_=u[:], func=ACT.Abs_reciprocal_sqrt, bias=c_pos[:]
-            )
+            sumsq[i] = u
+
+        def rsqrt(i):
+            r = small.tile([P, 2 * H], F32, name="r")
+            nc.scalar.activation(out=r[:], in_=sumsq[i][:], func=ACT.Abs_reciprocal_sqrt, bias=c_pos[:])
             rnorm[i] = r
 
-        def scale_on_scalar(i):
-            for g in range(V_GROUPS, 2 * H):
-                view = target(i, g // H)[:, g % H, :]
-                nc.scalar.activation(out=view, in_=view, func=ACT.Copy, scale=rnorm[i][:, g // H, g % H:g % H + 1])
-
-        def scale_on_vector(i):
-            for g in range(V_GROUPS):
-                view = target(i, g // H)[:, g % H, :]
-                nc.vector.tensor_scalar_mul(out=view, in0=view, scalar1=rnorm[i][:, g // H, g % H:g % H + 1])
+        def scale(i):
+            groups = stage[i // T][0][:].rearrange("p s h t d -> p (s h) t d")[:, :, i % T, :]
+            r = rnorm[i]
+            nv = V_GROUPS if i < NT - LAG else 2 * H
+            ns = S_GROUPS if i < NT - LAG else 0
+            for g in range(nv):
+                nc.vector.tensor_scalar_mul(out=groups[:, g, :], in0=groups[:, g, :], scalar1=r[:, g:g + 1])
+            for g in range(nv, nv + ns):
+                nc.scalar.activation(out=groups[:, g, :], in_=groups[:, g, :], func=ACT.Copy, scale=r[:, g:g + 1])
+            g0 = nv + ns
+            if g0 < 2 * H:
+                nc.gpsimd.tensor_tensor(
+                    out=groups[:, g0:, :], in0=groups[:, g0:, :],
+                    in1=r[:, g0:].unsqueeze(2).to_broadcast([P, 2 * H - g0, HD]), op=ALU.mult,
+                )
 
         block_end = {}
         i0 = 0
@@ -220,27 +230,33 @@ def tile_selfattention_pa_t_kernel(tc, x, W, b, out_0, out_1, out_2):
                     gx[pi] = x_grouped(pi, "s")
             for i in range(FIRST):
                 one_pass(i, s)
-                if s == 1:
-                    norms(i)
-                    scale_on_scalar(i)
-                if s == 2:
-                    scale_on_vector(i)
-                    if i % 2 == 1:
-                        x_quantise((FIRST + i) // 2, gx[(FIRST + i) // 2])
-        store(FIRST - 1, (2, 0, 1))
+                if s == 2 and i % 2 == 1:
+                    x_quantise((FIRST + i) // 2, gx[(FIRST + i) // 2])
+        for i in range(FIRST):
+            clamp(i)
+        for i in range(FIRST - 1):
+            rsqrt(i)
+        store(FIRST - 1, (2,))
 
-        for i in range(FIRST, NT + V_LAG):
+        scaled = 0
+        for i in range(FIRST, NT + LAG):
             if i < NT:
                 pi = i // 2 + AHEAD
                 if i % 2 == 0 and 2 * pi < NT:
                     gx[pi] = x_grouped(pi, "s")
-                for s in range(3):
-                    one_pass(i, s)
-                norms(i)
-                scale_on_scalar(i)
+                one_pass(i, 0)
+                if i > FIRST:
+                    clamp(i - 1)
+                one_pass(i, 1)
+                rsqrt(i - 1)
+                one_pass(i, 2)
                 store(i, (2,))
                 if i % 2 == 1 and 2 * pi < NT:
                     x_quantise(pi, gx[pi])
-            if i - V_LAG >= FIRST:
-                scale_on_vector(i - V_LAG)
-                store(i - V_LAG, (0, 1))
+            if i == NT:
+                clamp(i - 1)
+                rsqrt(i - 1)
+            while scaled <= min(i - LAG, NT - 1):
+                scale(scaled)
+                store(scaled, (0, 1))
+                scaled += 1

@@ -25,7 +25,7 @@ V_GROUPS = 2
 S_GROUPS = 0
 LAG = 2
 RING = 8
-BLOCKS = [4, 4, 4, 4, 4, 4, 4, 2, 1, 1]
+BLOCKS = [4, 4, 4, 4, 4, 4, 2, 2, 2, 1, 1]
 
 
 def tile_selfattention_pa_t_kernel(tc, x, W, b, out_0, out_1, out_2):
@@ -43,14 +43,17 @@ def tile_selfattention_pa_t_kernel(tc, x, W, b, out_0, out_1, out_2):
 
         w_sb = const.tile([P, 3, H, E], BF16)
         x_sb = const.tile([P, B, T, E], BF16)
-        b_row = const.tile([P, 3 * E], BF16)
+        b_rows = const.tile([P, 3 * HD], BF16)
         bias = const.tile([P, 3, H, HD], BF16)
-        ones = const.tile([P, P], BF16)
+        ident_b = const.tile([P, P], BF16)
         ident = const.tile([P, P], F32)
         c_pos = const.tile([P, 1], F32)
         c_neg = const.tile([P, 1], F32)
         warm = const.tile([P, 1], F32)
         junk = const.tile([P, RING, HD], BF16)
+        first_ss = const.tile([P, 2, FIRST, H], F32)
+        first_u = const.tile([P, 2, FIRST * H], F32)
+        first_r = const.tile([P, 2, FIRST * H], F32)
         w_codes = const.tile([P, 3, E], U32, align_bytes=64)
         w_scales = const.tile([P, 3, E], U8, align_bytes=64)
         w_view = W.rearrange("(h s p) k -> s p h k", h=H, s=3)
@@ -61,12 +64,9 @@ def tile_selfattention_pa_t_kernel(tc, x, W, b, out_0, out_1, out_2):
                 in_=x[bi].rearrange("(p t) k -> p t k", t=T)[:, t0:t1, :],
             )
 
-        nc.vector.memset(b_row[:], 0.0)
-        nc.scalar.dma_start(
-            out=b_row[0:1, :].rearrange("o (s h d) -> o s h d", s=3, h=H),
-            in_=b.rearrange("(o h s d) -> o s h d", o=1, h=H, s=3),
-        )
+        nc.vector.memset(b_rows[:].bitcast(U32), 0)
         load_x(0, 0, 2)
+        nc.sync.dma_start(out=b_rows[0:H, :], in_=b.rearrange("(h c) -> h c", h=H))
         nc.sync.dma_start(out=w_sb[:, 0, 0:2, :], in_=w_view[0][:, 0:2, :])
         nc.sync.dma_start(out=w_sb[:, 0, 2:4, :], in_=w_view[0][:, 2:4, :])
         load_x(0, 2, 4)
@@ -77,7 +77,7 @@ def tile_selfattention_pa_t_kernel(tc, x, W, b, out_0, out_1, out_2):
             load_x(bi, 0, T)
 
         make_identity(nc, ident[:])
-        nc.vector.memset(ones[:], 1.0)
+        make_identity(nc, ident_b[:])
         nc.vector.memset(c_pos[:], EPS * EPS)
         nc.vector.memset(c_neg[:], -EPS * EPS)
         nc.scalar.activation(out=warm[:], in_=c_pos[:], func=ACT.Abs_reciprocal_sqrt)
@@ -151,13 +151,17 @@ def tile_selfattention_pa_t_kernel(tc, x, W, b, out_0, out_1, out_2):
             nc.vector.tensor_tensor(out=target(i, s), in0=acc[:], in1=bias[:, s], op=ALU.add)
             if s == 2:
                 return
-            if i not in sumsq:
-                ss = small.tile([P, 2, H], F32, name="ss")
-                sumsq[i] = ss
+            if i < FIRST:
+                ss = first_ss[:, s, i, :]
+            else:
+                if i not in sumsq:
+                    ss_tile = small.tile([P, 2, H], F32, name="ss")
+                    sumsq[i] = ss_tile
+                ss = sumsq[i][:, s, :]
             for h in range(H):
                 nc.scalar.activation(
                     out=junk[:, (s * H + h) % RING, :], in_=target(i, s)[:, h, :], func=ACT.Square,
-                    accum_out=sumsq[i][:, s, h:h + 1],
+                    accum_out=ss[:, h:h + 1],
                 )
 
         def clamp(i):
@@ -169,6 +173,21 @@ def tile_selfattention_pa_t_kernel(tc, x, W, b, out_0, out_1, out_2):
             r = small.tile([P, 2 * H], F32, name="r")
             nc.scalar.activation(out=r[:], in_=sumsq[i][:], func=ACT.Abs_reciprocal_sqrt, bias=c_pos[:])
             rnorm[i] = r
+
+        def first_clamp(s):
+            nc.scalar.activation(
+                out=first_u[:, s], in_=first_ss[:, s].rearrange("p i h -> p (i h)"), func=ACT.Relu, bias=c_neg[:]
+            )
+
+        def first_rsqrt(s):
+            nc.scalar.activation(out=first_r[:, s], in_=first_u[:, s], func=ACT.Abs_reciprocal_sqrt, bias=c_pos[:])
+
+        def first_scale(s):
+            for i in range(FIRST):
+                r = first_r[:, s, i * H:(i + 1) * H]
+                nc.gpsimd.tensor_tensor(
+                    out=target(i, s), in0=target(i, s), in1=r.unsqueeze(2).to_broadcast([P, H, HD]), op=ALU.mult
+                )
 
         def scale(i):
             groups = stage[i // T][0][:].rearrange("p s h t d -> p (s h) t d")[:, :, i % T, :]
@@ -204,41 +223,40 @@ def tile_selfattention_pa_t_kernel(tc, x, W, b, out_0, out_1, out_2):
                     out=outs[s][bi].rearrange("h (p t) d -> p h t d", t=T)[:, :, t0:t0 + n, :], in_=src
                 )
 
-        for s in range(3):
+        def spread_bias(s):
             pb = ps_a.tile([P, H, HD], F32, name="acc")
-            nc.tensor.matmul(
-                out=pb[:].rearrange("p h d -> p (h d)"), lhsT=ones[:], rhs=b_row[:, s * E:(s + 1) * E],
-                start=True, stop=True,
-            )
-            if s == 1:
-                nc.vector.tensor_copy(out=bias[:, s], in_=pb[:])
-            else:
-                nc.scalar.copy(out=bias[:, s], in_=pb[:])
+            for h in range(H):
+                nc.tensor.matmul(
+                    out=pb[:, h, :], lhsT=ident_b[:, h:h + 1].to_broadcast([P, P]), rhs=b_rows[:, s * HD:(s + 1) * HD],
+                    start=True, stop=True,
+                )
+            nc.scalar.copy(out=bias[:, s], in_=pb[:])
 
         gx = {0: x_grouped(0, "v")}
         gw = w_grouped(0, "sv")
         x_quantise(0, gx[0])
+        for s in range(3):
+            spread_bias(s)
         gx[1] = x_grouped(1, "s")
         for s in range(3):
             w_quantise(s, gw)
-            if s == 0:
-                x_quantise(1, gx[1])
             if s < 2:
-                gw = w_grouped(s + 1, "ss")
-            else:
-                for pi in range(FIRST // 2, FIRST // 2 + AHEAD):
-                    gx[pi] = x_grouped(pi, "s")
+                gw = w_grouped(s + 1, "sv")
+            if s > 0:
+                gx[FIRST // 2 + s - 1] = x_grouped(FIRST // 2 + s - 1, "s")
+                first_clamp(s - 1)
             for i in range(FIRST):
                 one_pass(i, s)
+                if i == 1 and s == 0:
+                    x_quantise(1, gx[1])
+                if i == 0 and s > 0:
+                    first_rsqrt(s - 1)
+                    first_scale(s - 1)
                 if s == 2 and i % 2 == 1:
                     x_quantise((FIRST + i) // 2, gx[(FIRST + i) // 2])
-        for i in range(FIRST):
-            clamp(i)
-        for i in range(FIRST - 1):
-            rsqrt(i)
-        store(FIRST - 1, (2,))
+        store(FIRST - 1, (2, 0, 1))
 
-        scaled = 0
+        scaled = FIRST
         for i in range(FIRST, NT + LAG):
             if i < NT:
                 pi = i // 2 + AHEAD
@@ -248,7 +266,8 @@ def tile_selfattention_pa_t_kernel(tc, x, W, b, out_0, out_1, out_2):
                 if i > FIRST:
                     clamp(i - 1)
                 one_pass(i, 1)
-                rsqrt(i - 1)
+                if i > FIRST:
+                    rsqrt(i - 1)
                 one_pass(i, 2)
                 store(i, (2,))
                 if i % 2 == 1 and 2 * pi < NT:

@@ -21,8 +21,8 @@ FLOPS = 2 * B * L * E * 3 * E
 
 FIRST = 4
 AHEAD = 2
-V_GROUPS = 2
-S_GROUPS = 0
+V_GROUPS = 0
+S_GROUPS = 2
 LAG = 2
 RING = 8
 BLOCKS = [4, 4, 4, 4, 4, 4, 2, 2, 2, 1, 1]
@@ -261,7 +261,7 @@ def tile_selfattention_pa_t_kernel(tc, x, W, b, out_0, out_1, out_2):
             if i < NT:
                 pi = i // 2 + AHEAD
                 if i % 2 == 0 and 2 * pi < NT:
-                    gx[pi] = x_grouped(pi, "s")
+                    gx[pi] = x_grouped(pi, "sv"[pi % 2])
                 one_pass(i, 0)
                 if i > FIRST:
                     clamp(i - 1)

@@ -60,8 +60,8 @@ def tile_selfattention_pa_t_kernel(tc, x, W, b, out_0, out_1, out_2):
 
         def load_x(bi, t0, t1):
             nc.sync.dma_start(
-                out=x_sb[:, bi, t0:t1, :],
-                in_=x[bi].rearrange("(p t) k -> p t k", t=T)[:, t0:t1, :],
+                out=x_sb[:, bi].rearrange("p t k -> p (t k)")[:, t0 * E:t1 * E],
+                in_=x[bi].rearrange("(p t) k -> p (t k)", t=T)[:, t0 * E:t1 * E],
             )
 
         nc.vector.memset(b_rows[:].bitcast(U32), 0)
@@ -218,9 +218,11 @@ def tile_selfattention_pa_t_kernel(tc, x, W, b, out_0, out_1, out_2):
             bi, t0 = i // T, i % T - n + 1
             st_qk, st_v = stage[bi]
             for s in s_list:
-                src = st_v[:, :, t0:t0 + n, :] if s == 2 else st_qk[:, s, :, t0:t0 + n, :]
+                src = st_v[:] if s == 2 else st_qk[:, s]
+                run = slice(t0 * HD, (t0 + n) * HD)
                 nc.sync.dma_start(
-                    out=outs[s][bi].rearrange("h (p t) d -> p h t d", t=T)[:, :, t0:t0 + n, :], in_=src
+                    out=outs[s][bi].rearrange("h (p t) d -> p h (t d)", t=T)[:, :, run],
+                    in_=src.rearrange("p h t d -> p h (t d)")[:, :, run],
                 )
 
         def spread_bias(s):

@@ -19,13 +19,24 @@ NT = B * T
 EPS = 1e-12
 FLOPS = 2 * B * L * E * 3 * E
 
-FIRST = 4
-AHEAD = 2
-V_GROUPS = 0
-S_GROUPS = 2
-LAG = 2
-RING = 8
-BLOCKS = [4, 4, 4, 4, 4, 4, 2, 2, 2, 1, 1]
+SIZES = [4] * 8
+NB = len(SIZES)
+START = [sum(SIZES[:n]) for n in range(NB)]
+BLK = max(SIZES)
+G_HEADS = 3
+S_HEADS = 1
+RING = 32
+XE = ["vv", "vv"]
+QPOS = (1, 3)
+TG = (0, 0)
+TS = (0, 1)
+ORD = [(0, 1, 2)] * 16
+WC = ["sv", "sv", "sv"]
+HX = "ssss"
+GSPLIT = 1
+TAIL = 4
+CT = ((0, 0), (1, 1))
+QZ = 3
 
 
 def tile_selfattention_pa_t_kernel(tc, x, W, b, out_0, out_1, out_2):
@@ -34,8 +45,8 @@ def tile_selfattention_pa_t_kernel(tc, x, W, b, out_0, out_1, out_2):
     with ExitStack() as ctx:
         ctx.enter_context(tc.manual_schedule())
         const = ctx.enter_context(tc.tile_pool(name="const", bufs=1))
-        grp = ctx.enter_context(tc.tile_pool(name="grp", bufs=4))
-        cod = ctx.enter_context(tc.tile_pool(name="cod", bufs=5))
+        grp = ctx.enter_context(tc.tile_pool(name="grp", bufs=2))
+        cod = ctx.enter_context(tc.tile_pool(name="cod", bufs=3))
         stg = ctx.enter_context(tc.tile_pool(name="stg", bufs=3))
         small = ctx.enter_context(tc.tile_pool(name="small", bufs=6))
         ps_t = ctx.enter_context(tc.psum_pool(name="ps_t", bufs=2))
@@ -51,9 +62,6 @@ def tile_selfattention_pa_t_kernel(tc, x, W, b, out_0, out_1, out_2):
         c_neg = const.tile([P, 1], F32)
         warm = const.tile([P, 1], F32)
         junk = const.tile([P, RING, HD], BF16)
-        first_ss = const.tile([P, 2, FIRST, H], F32)
-        first_u = const.tile([P, 2, FIRST * H], F32)
-        first_r = const.tile([P, 2, FIRST * H], F32)
         w_codes = const.tile([P, 3, E], U32, align_bytes=64)
         w_scales = const.tile([P, 3, E], U8, align_bytes=64)
         w_view = W.rearrange("(h s p) k -> s p h k", h=H, s=3)
@@ -90,57 +98,64 @@ def tile_selfattention_pa_t_kernel(tc, x, W, b, out_0, out_1, out_2):
                     nc.tensor.transpose(bank[:, i, u, :], words[:, u * P:(u + 1) * P], ident[:])
             return bank
 
-        def copy_out(bank, engine):
-            g = grp.tile([P, 2 * E], BF16, name="g", align_bytes=64)
-            dst = g[:].bitcast(F32).rearrange("p (i r u) -> p i r u", i=2, u=2)
+        def copy_out(bank, dst, engine):
+            dst = dst.bitcast(F32).rearrange("p (i r u) -> p i r u", i=2, u=2)
             src = bank[:].rearrange("p i u r -> p i r u")
             if engine == "v":
                 nc.vector.tensor_copy(out=dst, in_=src)
             else:
                 nc.scalar.copy(out=dst, in_=src)
-            return g
 
         def quantise(g, codes, scales):
-            nc.vector.quantize_mx(out=codes.bitcast(FP8X4), scales=scales, in_=g[:])
+            nc.vector.quantize_mx(out=codes.bitcast(FP8X4), scales=scales, in_=g)
 
         def w_grouped(s, engines):
             banks = [transposes([w_sb[:, s, 2 * a + i, :] for i in range(2)], ps_a, "acc") for a in range(2)]
-            return [copy_out(banks[a], engines[a]) for a in range(2)]
-
-        def w_quantise(s, gs):
+            gw = grp.tile([P, 4 * E], BF16, name="gw", align_bytes=64)
             for a in range(2):
-                cols = slice(a * 2 * P, (a + 1) * 2 * P)
-                quantise(gs[a], w_codes[:, s, cols], w_scales[:, s, cols])
+                copy_out(banks[a], gw[:, a * 2 * E:(a + 1) * 2 * E], engines[a])
+            return gw
 
-        def x_grouped(pi, engine):
-            rows = [x_sb[:, (2 * pi + j) // T, (2 * pi + j) % T, :] for j in range(2)]
-            return copy_out(transposes(rows, ps_t, "pt"), engine)
+        def w_quantise(s, gw):
+            quantise(gw[:], w_codes[:, s, :], w_scales[:, s, :])
 
         x_mx = {}
 
-        def x_quantise(pi, g):
-            xc = cod.tile([P, 2 * P], U32, name="xc", align_bytes=64)
-            xs = cod.tile([P, 2 * P], U8, name="xs", align_bytes=64)
-            quantise(g, xc[:], xs[:])
-            x_mx[pi] = (xc, xs)
+        def x_block(n):
+            if n not in x_mx:
+                gx = grp.tile([P, BLK * E], BF16, name="gx", align_bytes=64)
+                xc = cod.tile([P, BLK * P], U32, name="xc", align_bytes=64)
+                xs = cod.tile([P, BLK * P], U8, name="xs", align_bytes=64)
+                x_mx[n] = (gx, xc, xs)
+            return x_mx[n]
+
+        def x_grouped(n, t, engine):
+            gx = x_block(n)[0]
+            rows = [x_sb[:, START[n] // T, START[n] % T + t + j, :] for j in range(2)]
+            copy_out(transposes(rows, ps_t, "pt"), gx[:, t * E:(t + 2) * E], engine)
+
+        def x_quantise(n, t, size):
+            gx, xc, xs = x_block(n)
+            quantise(gx[:, t * E:(t + size) * E], xc[:, t * P:(t + size) * P], xs[:, t * P:(t + size) * P])
 
         stage = {}
         sumsq = {}
         rnorm = {}
 
-        def target(i, s):
-            st_qk, st_v = stage[i // T]
-            if s == 2:
-                return st_v[:, :, i % T, :]
-            return st_qk[:, s, :, i % T, :]
-
-        def one_pass(i, s):
-            if i // T not in stage:
+        def target(n, s):
+            if START[n] // T not in stage:
                 st_qk = stg.tile([P, 2, H, T, HD], F32, name="st_qk")
                 st_v = stg.tile([P, H, T, HD], F32, name="st_v")
-                stage[i // T] = (st_qk, st_v)
-            xc, xs = x_mx[i // 2]
-            cols = slice((i % 2) * P, (i % 2 + 1) * P)
+                stage[START[n] // T] = (st_qk, st_v)
+            st_qk, st_v = stage[START[n] // T]
+            t0 = START[n] % T
+            if s == 2:
+                return st_v[:, :, t0:t0 + SIZES[n], :]
+            return st_qk[:, s, :, t0:t0 + SIZES[n], :]
+
+        def multiply(n, s, t):
+            gx, xc, xs = x_mx[n]
+            cols = slice(t * P, (t + 1) * P)
             acc = ps_a.tile([P, H, HD], F32, name="acc")
             nc.tensor.matmul_mx(
                 out=acc[:].rearrange("p h d -> p (h d)"),
@@ -148,82 +163,67 @@ def tile_selfattention_pa_t_kernel(tc, x, W, b, out_0, out_1, out_2):
                 rhs=w_codes[:, s, :].bitcast(FP8X4), rhs_scale=w_scales[:, s, :],
                 start=True, stop=True,
             )
-            nc.vector.tensor_tensor(out=target(i, s), in0=acc[:], in1=bias[:, s], op=ALU.add)
-            if s == 2:
-                return
-            if i < FIRST:
-                ss = first_ss[:, s, i, :]
-            else:
-                if i not in sumsq:
-                    ss_tile = small.tile([P, 2, H], F32, name="ss")
-                    sumsq[i] = ss_tile
-                ss = sumsq[i][:, s, :]
+            return acc
+
+        def add_bias(n, s, t, acc):
+            nc.vector.tensor_tensor(out=target(n, s)[:, :, t, :], in0=bias[:, s], in1=acc[:], op=ALU.add)
+
+        def squares(n, s, t):
+            if n not in sumsq:
+                ss = small.tile([P, 2, H, SIZES[n]], F32, name="ss")
+                sumsq[n] = ss
             for h in range(H):
                 nc.scalar.activation(
-                    out=junk[:, (s * H + h) % RING, :], in_=target(i, s)[:, h, :], func=ACT.Square,
-                    accum_out=ss[:, h:h + 1],
+                    out=junk[:, (t * H + h + s * BLK * H) % RING, :], in_=target(n, s)[:, h, t, :], func=ACT.Square,
+                    accum_out=sumsq[n][:, s, h, t:t + 1],
                 )
 
-        def clamp(i):
-            u = small.tile([P, 2 * H], F32, name="u")
-            nc.scalar.activation(out=u[:], in_=sumsq[i][:].rearrange("p s h -> p (s h)"), func=ACT.Relu, bias=c_neg[:])
-            sumsq[i] = u
-
-        def rsqrt(i):
-            r = small.tile([P, 2 * H], F32, name="r")
-            nc.scalar.activation(out=r[:], in_=sumsq[i][:], func=ACT.Abs_reciprocal_sqrt, bias=c_pos[:])
-            rnorm[i] = r
-
-        def first_clamp(s):
+        def clamp(n, s):
+            if n not in rnorm:
+                u = small.tile([P, 2, H * SIZES[n]], F32, name="u")
+                r = small.tile([P, 2, H, SIZES[n]], F32, name="r")
+                rnorm[n] = (u, r)
             nc.scalar.activation(
-                out=first_u[:, s], in_=first_ss[:, s].rearrange("p i h -> p (i h)"), func=ACT.Relu, bias=c_neg[:]
+                out=rnorm[n][0][:, s], in_=sumsq[n][:, s].rearrange("p h t -> p (h t)"), func=ACT.Relu, bias=c_neg[:]
             )
 
-        def first_rsqrt(s):
-            nc.scalar.activation(out=first_r[:, s], in_=first_u[:, s], func=ACT.Abs_reciprocal_sqrt, bias=c_pos[:])
+        def rsqrt(n, s):
+            u, r = rnorm[n]
+            nc.scalar.activation(
+                out=r[:, s].rearrange("p h t -> p (h t)"), in_=u[:, s], func=ACT.Abs_reciprocal_sqrt, bias=c_pos[:]
+            )
 
-        def first_scale(s):
-            for i in range(FIRST):
-                r = first_r[:, s, i * H:(i + 1) * H]
-                nc.gpsimd.tensor_tensor(
-                    out=target(i, s), in0=target(i, s), in1=r.unsqueeze(2).to_broadcast([P, H, HD]), op=ALU.mult
-                )
-
-        def scale(i):
-            groups = stage[i // T][0][:].rearrange("p s h t d -> p (s h) t d")[:, :, i % T, :]
-            r = rnorm[i]
-            nv = V_GROUPS if i < NT - LAG else 2 * H
-            ns = S_GROUPS if i < NT - LAG else 0
-            for g in range(nv):
-                nc.vector.tensor_scalar_mul(out=groups[:, g, :], in0=groups[:, g, :], scalar1=r[:, g:g + 1])
-            for g in range(nv, nv + ns):
-                nc.scalar.activation(out=groups[:, g, :], in_=groups[:, g, :], func=ACT.Copy, scale=r[:, g:g + 1])
-            g0 = nv + ns
-            if g0 < 2 * H:
-                nc.gpsimd.tensor_tensor(
-                    out=groups[:, g0:, :], in0=groups[:, g0:, :],
-                    in1=r[:, g0:].unsqueeze(2).to_broadcast([P, 2 * H - g0, HD]), op=ALU.mult,
-                )
-
-        block_end = {}
-        i0 = 0
-        for n in BLOCKS:
-            block_end[i0 + n - 1] = n
-            i0 += n
-
-        def store(i, s_list):
-            if i not in block_end:
+        def scale_g(n, s, heads):
+            y, r = target(n, s), rnorm[n][1]
+            if heads == 0:
                 return
-            n = block_end[i]
-            bi, t0 = i // T, i % T - n + 1
-            st_qk, st_v = stage[bi]
-            for s in s_list:
-                src = st_v[:] if s == 2 else st_qk[:, s]
-                run = slice(t0 * HD, (t0 + n) * HD)
-                nc.sync.dma_start(
-                    out=outs[s][bi].rearrange("h (p t) d -> p h (t d)", t=T)[:, :, run],
-                    in_=src.rearrange("p h t d -> p h (t d)")[:, :, run],
+            w = SIZES[n] // GSPLIT
+            for t0 in range(0, SIZES[n], w):
+                nc.gpsimd.tensor_tensor(
+                    out=y[:, :heads, t0:t0 + w, :], in0=y[:, :heads, t0:t0 + w, :],
+                    in1=r[:, s, :heads, t0:t0 + w].unsqueeze(3).to_broadcast([P, heads, w, HD]), op=ALU.mult,
                 )
+
+        def scale_s(n, s, h0, h1):
+            y, r = target(n, s), rnorm[n][1]
+            for h in range(h0, h1):
+                for t in range(SIZES[n]):
+                    nc.scalar.activation(out=y[:, h, t, :], in_=y[:, h, t, :], func=ACT.Copy, scale=r[:, s, h, t:t + 1])
+
+        def scale_v(n, s, h0, h1):
+            y, r = target(n, s), rnorm[n][1]
+            for t in range(SIZES[n]):
+                for h in range(h0, h1):
+                    nc.vector.tensor_scalar_mul(out=y[:, h, t, :], in0=y[:, h, t, :], scalar1=r[:, s, h, t:t + 1])
+
+        def store(n, s):
+            bi, t = START[n] // T, START[n] % T
+            run = slice(t * HD, (t + SIZES[n]) * HD)
+            st = stage[bi][1] if s == 2 else stage[bi][0][:, s]
+            nc.sync.dma_start(
+                out=outs[s][bi].rearrange("h (p t) d -> p h (t d)", t=T)[:, :, run],
+                in_=(st[:] if s == 2 else st).rearrange("p h t d -> p h (t d)")[:, :, run],
+            )
 
         def spread_bias(s):
             pb = ps_a.tile([P, H, HD], F32, name="acc")
@@ -234,50 +234,59 @@ def tile_selfattention_pa_t_kernel(tc, x, W, b, out_0, out_1, out_2):
                 )
             nc.scalar.copy(out=bias[:, s], in_=pb[:])
 
-        gx = {0: x_grouped(0, "v")}
-        gw = w_grouped(0, "sv")
-        x_quantise(0, gx[0])
-        for s in range(3):
-            spread_bias(s)
-        gx[1] = x_grouped(1, "s")
-        for s in range(3):
-            w_quantise(s, gw)
-            if s < 2:
-                gw = w_grouped(s + 1, "sv")
-            if s > 0:
-                gx[FIRST // 2 + s - 1] = x_grouped(FIRST // 2 + s - 1, "s")
-                first_clamp(s - 1)
-            for i in range(FIRST):
-                one_pass(i, s)
-                if i == 1 and s == 0:
-                    x_quantise(1, gx[1])
-                if i == 0 and s > 0:
-                    first_rsqrt(s - 1)
-                    first_scale(s - 1)
-                if s == 2 and i % 2 == 1:
-                    x_quantise((FIRST + i) // 2, gx[(FIRST + i) // 2])
-        store(FIRST - 1, (2, 0, 1))
+        def finish(n, s):
+            last = START[n] >= NT - TAIL
+            g = TG[s] if last else G_HEADS
+            sc = TS[s] if last else S_HEADS
+            scale_g(n, s, g)
+            scale_s(n, s, g, g + sc)
+            scale_v(n, s, g + sc, H)
+            store(n, s)
 
-        scaled = FIRST
-        for i in range(FIRST, NT + LAG):
-            if i < NT:
-                pi = i // 2 + AHEAD
-                if i % 2 == 0 and 2 * pi < NT:
-                    gx[pi] = x_grouped(pi, "sv"[pi % 2])
-                one_pass(i, 0)
-                if i > FIRST:
-                    clamp(i - 1)
-                one_pass(i, 1)
-                if i > FIRST:
-                    rsqrt(i - 1)
-                one_pass(i, 2)
-                store(i, (2,))
-                if i % 2 == 1 and 2 * pi < NT:
-                    x_quantise(pi, gx[pi])
-            if i == NT:
-                clamp(i - 1)
-                rsqrt(i - 1)
-            while scaled <= min(i - LAG, NT - 1):
-                scale(scaled)
-                store(scaled, (0, 1))
-                scaled += 1
+        todo = []
+        for n in range(NB):
+            order = ORD[n]
+            if n == 0:
+                x_grouped(0, 0, "v")
+                gw = w_grouped(order[0], "sv")
+                x_quantise(0, 0, 2)
+                for s in order:
+                    spread_bias(s)
+                if SIZES[0] == 4:
+                    x_grouped(0, 2, HX[1])
+            nt = SIZES[n]
+            for j in range(3):
+                s = order[j]
+                if n == 0:
+                    w_quantise(s, gw)
+                    if j == 0 and nt == 4:
+                        x_quantise(0, 2, 2)
+                    if j > 0 and 2 * j - 2 < SIZES[1]:
+                        x_grouped(1, 2 * j - 2, HX[1 + j])
+                    if j < 2:
+                        gw = w_grouped(order[j + 1], WC[j])
+                elif j == 0 and n + 1 < NB:
+                    for a in range(SIZES[n + 1] // 2):
+                        x_grouped(n + 1, 2 * a, XE[n % 2][a])
+                for t in range(nt):
+                    add_bias(n, s, t, multiply(n, s, t))
+                    if (j, t) == (QPOS[0], min(QPOS[1], nt - 1)) and n > 0 and n + 1 < NB:
+                        x_quantise(n + 1, 0, SIZES[n + 1])
+                    if n == 0 and j == 1 and t == nt - 1 and SIZES[1] == 2 or n == 0 and j == 2 and t == QZ and SIZES[1] == 4:
+                        x_quantise(1, 0, SIZES[1])
+                    if s < 2:
+                        squares(n, s, t)
+                    if t == CT[0][nt // 4] and todo:
+                        clamp(*todo[0])
+                    if t == CT[1][nt // 4] and todo:
+                        rsqrt(*todo[0])
+                    if t == nt - 1 and s == 2:
+                        store(n, 2)
+                    if t == nt - 1 and todo:
+                        finish(*todo.pop(0))
+                if s < 2:
+                    todo.append((n, s))
+        for n, s in todo:
+            clamp(n, s)
+            rsqrt(n, s)
+            finish(n, s)

@@ -13,30 +13,14 @@ ALU = mybir.AluOpType
 
 B, L, E, H = 4, 1024, 512, 4
 HD = E // H
+Q, K, V = 0, 1, 2
 P = 128
 T = L // P
-NT = B * T
+BLOCK = 4
+NB = B * T // BLOCK
 EPS = 1e-12
 FLOPS = 2 * B * L * E * 3 * E
-
-SIZES = [4] * 8
-NB = len(SIZES)
-START = [sum(SIZES[:n]) for n in range(NB)]
-BLK = max(SIZES)
-G_HEADS = 3
-S_HEADS = 1
 RING = 32
-XE = ["vv", "vv"]
-QPOS = (1, 3)
-TG = (0, 0)
-TS = (0, 1)
-ORD = [(0, 1, 2)] * 16
-WC = ["sv", "sv", "sv"]
-HX = "ssss"
-GSPLIT = 1
-TAIL = 4
-CT = ((0, 0), (1, 1))
-QZ = 3
 
 
 def tile_selfattention_pa_t_kernel(tc, x, W, b, out_0, out_1, out_2):
@@ -64,7 +48,6 @@ def tile_selfattention_pa_t_kernel(tc, x, W, b, out_0, out_1, out_2):
         junk = const.tile([P, RING, HD], BF16)
         w_codes = const.tile([P, 3, E], U32, align_bytes=64)
         w_scales = const.tile([P, 3, E], U8, align_bytes=64)
-        w_view = W.rearrange("(h s p) k -> s p h k", h=H, s=3)
 
         def load_x(bi, t0, t1):
             nc.sync.dma_start(
@@ -72,14 +55,18 @@ def tile_selfattention_pa_t_kernel(tc, x, W, b, out_0, out_1, out_2):
                 in_=x[bi].rearrange("(p t) k -> p (t k)", t=T)[:, t0 * E:t1 * E],
             )
 
+        def load_w(s, h0, h1):
+            rows = W.rearrange("(h s p) k -> s p h k", h=H, s=3)
+            nc.sync.dma_start(out=w_sb[:, s, h0:h1, :], in_=rows[s][:, h0:h1, :])
+
         nc.vector.memset(b_rows[:].bitcast(U32), 0)
         load_x(0, 0, 2)
         nc.sync.dma_start(out=b_rows[0:H, :], in_=b.rearrange("(h c) -> h c", h=H))
-        nc.sync.dma_start(out=w_sb[:, 0, 0:2, :], in_=w_view[0][:, 0:2, :])
-        nc.sync.dma_start(out=w_sb[:, 0, 2:4, :], in_=w_view[0][:, 2:4, :])
+        load_w(Q, 0, 2)
+        load_w(Q, 2, 4)
         load_x(0, 2, 4)
-        nc.sync.dma_start(out=w_sb[:, 1], in_=w_view[1])
-        nc.sync.dma_start(out=w_sb[:, 2], in_=w_view[2])
+        load_w(K, 0, 4)
+        load_w(V, 0, 4)
         load_x(0, 4, T)
         for bi in range(1, B):
             load_x(bi, 0, T)
@@ -90,139 +77,125 @@ def tile_selfattention_pa_t_kernel(tc, x, W, b, out_0, out_1, out_2):
         nc.vector.memset(c_neg[:], -EPS * EPS)
         nc.scalar.activation(out=warm[:], in_=c_pos[:], func=ACT.Abs_reciprocal_sqrt)
 
-        def transposes(rows, pool, name):
+        def turn(tiles, pool, name, dst, engine):
             bank = pool.tile([P, 2, 2, P], F32, name=name)
             for i in range(2):
-                words = rows[i].bitcast(F32)
+                words = tiles[i].bitcast(F32)
                 for u in range(2):
                     nc.tensor.transpose(bank[:, i, u, :], words[:, u * P:(u + 1) * P], ident[:])
-            return bank
 
-        def copy_out(bank, dst, engine):
-            dst = dst.bitcast(F32).rearrange("p (i r u) -> p i r u", i=2, u=2)
-            src = bank[:].rearrange("p i u r -> p i r u")
-            if engine == "v":
-                nc.vector.tensor_copy(out=dst, in_=src)
-            else:
-                nc.scalar.copy(out=dst, in_=src)
+            def copy_out():
+                src = bank[:].rearrange("p i u r -> p i r u")
+                out = dst.bitcast(F32).rearrange("p (i r u) -> p i r u", i=2, u=2)
+                if engine == "vector":
+                    nc.vector.tensor_copy(out=out, in_=src)
+                else:
+                    nc.scalar.copy(out=out, in_=src)
+            return copy_out
 
-        def quantise(g, codes, scales):
-            nc.vector.quantize_mx(out=codes.bitcast(FP8X4), scales=scales, in_=g)
+        def quantise(values, codes, scales):
+            nc.vector.quantize_mx(out=codes.bitcast(FP8X4), scales=scales, in_=values)
 
-        def w_grouped(s, engines):
-            banks = [transposes([w_sb[:, s, 2 * a + i, :] for i in range(2)], ps_a, "acc") for a in range(2)]
-            gw = grp.tile([P, 4 * E], BF16, name="gw", align_bytes=64)
-            for a in range(2):
-                copy_out(banks[a], gw[:, a * 2 * E:(a + 1) * 2 * E], engines[a])
-            return gw
-
-        def w_quantise(s, gw):
-            quantise(gw[:], w_codes[:, s, :], w_scales[:, s, :])
+        def turn_w(s):
+            values = grp.tile([P, 4 * E], BF16, name="gw", align_bytes=64)
+            copies = []
+            for a, engine in ((0, "scalar"), (1, "vector")):
+                tiles = [w_sb[:, s, 2 * a + i, :] for i in range(2)]
+                copies.append(turn(tiles, ps_a, "acc", values[:, a * 2 * E:(a + 1) * 2 * E], engine))
+            for copy_out in copies:
+                copy_out()
+            return values
 
         x_mx = {}
 
-        def x_block(n):
+        def turn_x(n, t, engine):
             if n not in x_mx:
-                gx = grp.tile([P, BLK * E], BF16, name="gx", align_bytes=64)
-                xc = cod.tile([P, BLK * P], U32, name="xc", align_bytes=64)
-                xs = cod.tile([P, BLK * P], U8, name="xs", align_bytes=64)
-                x_mx[n] = (gx, xc, xs)
-            return x_mx[n]
+                values = grp.tile([P, BLOCK * E], BF16, name="gx", align_bytes=64)
+                codes = cod.tile([P, BLOCK * P], U32, name="xc", align_bytes=64)
+                scales = cod.tile([P, BLOCK * P], U8, name="xs", align_bytes=64)
+                x_mx[n] = (values, codes, scales)
+            first = n * BLOCK + t
+            tiles = [x_sb[:, (first + i) // T, (first + i) % T, :] for i in range(2)]
+            turn(tiles, ps_t, "pt", x_mx[n][0][:, t * E:(t + 2) * E], engine)()
 
-        def x_grouped(n, t, engine):
-            gx = x_block(n)[0]
-            rows = [x_sb[:, START[n] // T, START[n] % T + t + j, :] for j in range(2)]
-            copy_out(transposes(rows, ps_t, "pt"), gx[:, t * E:(t + 2) * E], engine)
-
-        def x_quantise(n, t, size):
-            gx, xc, xs = x_block(n)
-            quantise(gx[:, t * E:(t + size) * E], xc[:, t * P:(t + size) * P], xs[:, t * P:(t + size) * P])
+        def quantise_x(n, t0, t1):
+            values, codes, scales = x_mx[n]
+            quantise(values[:, t0 * E:t1 * E], codes[:, t0 * P:t1 * P], scales[:, t0 * P:t1 * P])
 
         stage = {}
         sumsq = {}
-        rnorm = {}
+        norms = {}
 
-        def target(n, s):
-            if START[n] // T not in stage:
+        def results(n, s):
+            bi, t0 = n * BLOCK // T, n * BLOCK % T
+            if bi not in stage:
                 st_qk = stg.tile([P, 2, H, T, HD], F32, name="st_qk")
                 st_v = stg.tile([P, H, T, HD], F32, name="st_v")
-                stage[START[n] // T] = (st_qk, st_v)
-            st_qk, st_v = stage[START[n] // T]
-            t0 = START[n] % T
-            if s == 2:
-                return st_v[:, :, t0:t0 + SIZES[n], :]
-            return st_qk[:, s, :, t0:t0 + SIZES[n], :]
+                stage[bi] = (st_qk, st_v)
+            whole = stage[bi][1][:] if s == V else stage[bi][0][:, s]
+            return whole[:, :, t0:t0 + BLOCK, :]
 
-        def multiply(n, s, t):
-            gx, xc, xs = x_mx[n]
+        def project(n, s, t):
+            values, codes, scales = x_mx[n]
             cols = slice(t * P, (t + 1) * P)
             acc = ps_a.tile([P, H, HD], F32, name="acc")
             nc.tensor.matmul_mx(
                 out=acc[:].rearrange("p h d -> p (h d)"),
-                lhsT=xc[:, cols].bitcast(FP8X4), lhsT_scale=xs[:, cols],
+                lhsT=codes[:, cols].bitcast(FP8X4), lhsT_scale=scales[:, cols],
                 rhs=w_codes[:, s, :].bitcast(FP8X4), rhs_scale=w_scales[:, s, :],
                 start=True, stop=True,
             )
-            return acc
-
-        def add_bias(n, s, t, acc):
-            nc.vector.tensor_tensor(out=target(n, s)[:, :, t, :], in0=bias[:, s], in1=acc[:], op=ALU.add)
+            nc.vector.tensor_tensor(out=results(n, s)[:, :, t, :], in0=bias[:, s], in1=acc[:], op=ALU.add)
 
         def squares(n, s, t):
             if n not in sumsq:
-                ss = small.tile([P, 2, H, SIZES[n]], F32, name="ss")
+                ss = small.tile([P, 2, H, BLOCK], F32, name="ss")
                 sumsq[n] = ss
             for h in range(H):
                 nc.scalar.activation(
-                    out=junk[:, (t * H + h + s * BLK * H) % RING, :], in_=target(n, s)[:, h, t, :], func=ACT.Square,
+                    out=junk[:, (s * BLOCK + t) * H + h, :], in_=results(n, s)[:, h, t, :], func=ACT.Square,
                     accum_out=sumsq[n][:, s, h, t:t + 1],
                 )
 
         def clamp(n, s):
-            if n not in rnorm:
-                u = small.tile([P, 2, H * SIZES[n]], F32, name="u")
-                r = small.tile([P, 2, H, SIZES[n]], F32, name="r")
-                rnorm[n] = (u, r)
+            if n not in norms:
+                u = small.tile([P, 2, H * BLOCK], F32, name="u")
+                r = small.tile([P, 2, H, BLOCK], F32, name="r")
+                norms[n] = (u, r)
             nc.scalar.activation(
-                out=rnorm[n][0][:, s], in_=sumsq[n][:, s].rearrange("p h t -> p (h t)"), func=ACT.Relu, bias=c_neg[:]
+                out=norms[n][0][:, s], in_=sumsq[n][:, s].rearrange("p h t -> p (h t)"), func=ACT.Relu, bias=c_neg[:]
             )
 
         def rsqrt(n, s):
-            u, r = rnorm[n]
+            u, r = norms[n]
             nc.scalar.activation(
                 out=r[:, s].rearrange("p h t -> p (h t)"), in_=u[:, s], func=ACT.Abs_reciprocal_sqrt, bias=c_pos[:]
             )
 
-        def scale_g(n, s, heads):
-            y, r = target(n, s), rnorm[n][1]
-            if heads == 0:
-                return
-            w = SIZES[n] // GSPLIT
-            for t0 in range(0, SIZES[n], w):
+        def scale(n, s, heads, engine):
+            y, r = results(n, s), norms[n][1]
+            h0, h1 = heads
+            if engine == "gpsimd" and h1 > h0:
                 nc.gpsimd.tensor_tensor(
-                    out=y[:, :heads, t0:t0 + w, :], in0=y[:, :heads, t0:t0 + w, :],
-                    in1=r[:, s, :heads, t0:t0 + w].unsqueeze(3).to_broadcast([P, heads, w, HD]), op=ALU.mult,
+                    out=y[:, h0:h1], in0=y[:, h0:h1],
+                    in1=r[:, s, h0:h1].unsqueeze(3).to_broadcast([P, h1 - h0, BLOCK, HD]), op=ALU.mult,
                 )
-
-        def scale_s(n, s, h0, h1):
-            y, r = target(n, s), rnorm[n][1]
-            for h in range(h0, h1):
-                for t in range(SIZES[n]):
-                    nc.scalar.activation(out=y[:, h, t, :], in_=y[:, h, t, :], func=ACT.Copy, scale=r[:, s, h, t:t + 1])
-
-        def scale_v(n, s, h0, h1):
-            y, r = target(n, s), rnorm[n][1]
-            for t in range(SIZES[n]):
+            elif engine == "scalar":
                 for h in range(h0, h1):
-                    nc.vector.tensor_scalar_mul(out=y[:, h, t, :], in0=y[:, h, t, :], scalar1=r[:, s, h, t:t + 1])
+                    for t in range(BLOCK):
+                        nc.scalar.activation(out=y[:, h, t, :], in_=y[:, h, t, :], func=ACT.Copy, scale=r[:, s, h, t:t + 1])
+            elif engine == "vector":
+                for t in range(BLOCK):
+                    for h in range(h0, h1):
+                        nc.vector.tensor_scalar_mul(out=y[:, h, t, :], in0=y[:, h, t, :], scalar1=r[:, s, h, t:t + 1])
 
         def store(n, s):
-            bi, t = START[n] // T, START[n] % T
-            run = slice(t * HD, (t + SIZES[n]) * HD)
-            st = stage[bi][1] if s == 2 else stage[bi][0][:, s]
+            bi, t0 = n * BLOCK // T, n * BLOCK % T
+            run = slice(t0 * HD, (t0 + BLOCK) * HD)
+            whole = stage[bi][1][:] if s == V else stage[bi][0][:, s]
             nc.sync.dma_start(
                 out=outs[s][bi].rearrange("h (p t) d -> p h (t d)", t=T)[:, :, run],
-                in_=(st[:] if s == 2 else st).rearrange("p h t d -> p h (t d)")[:, :, run],
+                in_=whole.rearrange("p h t d -> p h (t d)")[:, :, run],
             )
 
         def spread_bias(s):
@@ -234,59 +207,64 @@ def tile_selfattention_pa_t_kernel(tc, x, W, b, out_0, out_1, out_2):
                 )
             nc.scalar.copy(out=bias[:, s], in_=pb[:])
 
-        def finish(n, s):
-            last = START[n] >= NT - TAIL
-            g = TG[s] if last else G_HEADS
-            sc = TS[s] if last else S_HEADS
-            scale_g(n, s, g)
-            scale_s(n, s, g, g + sc)
-            scale_v(n, s, g + sc, H)
-            store(n, s)
+        waiting = []
+        held = []
 
-        todo = []
+        def finish(n, s):
+            if n == NB - 1:
+                g, a = 0, s
+            elif s == Q and n > 0 and n % 2 == 0:
+                g, a = H, H
+            else:
+                g, a = H - 1, H
+            scale(n, s, (0, g), "gpsimd")
+            scale(n, s, (g, a), "scalar")
+            scale(n, s, (a, H), "vector")
+            if s == Q and 0 < n < NB - 1:
+                held.append((n, s))
+            else:
+                store(n, s)
+
+        turn_x(0, 0, "vector")
+        w_values = turn_w(Q)
+        quantise_x(0, 0, 2)
+        spread_bias(Q)
+        turn_x(0, 2, "scalar")
+        spread_bias(K)
+        spread_bias(V)
         for n in range(NB):
-            order = ORD[n]
-            if n == 0:
-                x_grouped(0, 0, "v")
-                gw = w_grouped(order[0], "sv")
-                x_quantise(0, 0, 2)
-                for s in order:
-                    spread_bias(s)
-                if SIZES[0] == 4:
-                    x_grouped(0, 2, HX[1])
-            nt = SIZES[n]
+            order = (V, Q, K) if n == NB - 1 else (Q, K, V)
             for j in range(3):
                 s = order[j]
                 if n == 0:
-                    w_quantise(s, gw)
-                    if j == 0 and nt == 4:
-                        x_quantise(0, 2, 2)
-                    if j > 0 and 2 * j - 2 < SIZES[1]:
-                        x_grouped(1, 2 * j - 2, HX[1 + j])
+                    quantise(w_values[:], w_codes[:, s, :], w_scales[:, s, :])
+                    if j == 0:
+                        quantise_x(0, 2, 4)
+                    else:
+                        turn_x(1, 2 * j - 2, "vector")
                     if j < 2:
-                        gw = w_grouped(order[j + 1], WC[j])
+                        w_values = turn_w(order[j + 1])
                 elif j == 0 and n + 1 < NB:
-                    for a in range(SIZES[n + 1] // 2):
-                        x_grouped(n + 1, 2 * a, XE[n % 2][a])
-                for t in range(nt):
-                    add_bias(n, s, t, multiply(n, s, t))
-                    if (j, t) == (QPOS[0], min(QPOS[1], nt - 1)) and n > 0 and n + 1 < NB:
-                        x_quantise(n + 1, 0, SIZES[n + 1])
-                    if n == 0 and j == 1 and t == nt - 1 and SIZES[1] == 2 or n == 0 and j == 2 and t == QZ and SIZES[1] == 4:
-                        x_quantise(1, 0, SIZES[1])
-                    if s < 2:
+                    turn_x(n + 1, 0, "scalar" if n % 2 == 1 and n < NB - 2 else "vector")
+                    turn_x(n + 1, 2, "vector")
+                for t in range(BLOCK):
+                    project(n, s, t)
+                    if n + 1 < NB and (n, j, t) in ((0, 2, 2), (n, 0, 3)) and (n > 0 or j == 2):
+                        quantise_x(n + 1, 0, BLOCK)
+                    if s != V:
                         squares(n, s, t)
-                    if t == CT[0][nt // 4] and todo:
-                        clamp(*todo[0])
-                    if t == CT[1][nt // 4] and todo:
-                        rsqrt(*todo[0])
-                    if t == nt - 1 and s == 2:
-                        store(n, 2)
-                    if t == nt - 1 and todo:
-                        finish(*todo.pop(0))
-                if s < 2:
-                    todo.append((n, s))
-        for n, s in todo:
-            clamp(n, s)
-            rsqrt(n, s)
-            finish(n, s)
+                        if waiting and t == 0:
+                            clamp(*waiting[0])
+                        if waiting and t == 1:
+                            rsqrt(*waiting[0])
+                    elif t == BLOCK - 1:
+                        store(n, V)
+                        while held:
+                            store(*held.pop())
+                    if s != V and waiting and t == BLOCK - 1:
+                        finish(*waiting.pop(0))
+                if s != V:
+                    waiting.append((n, s))
+        clamp(*waiting[0])
+        rsqrt(*waiting[0])
+        finish(*waiting[0])

@@ -213,8 +213,6 @@ def tile_selfattention_pa_t_kernel(tc, x, W, b, out_0, out_1, out_2):
         def finish(n, s):
             if n == NB - 1:
                 g, a = 0, s
-            elif s == Q and n > 0 and n % 2 == 0:
-                g, a = H, H
             else:
                 g, a = H - 1, H
             scale(n, s, (0, g), "gpsimd")
@@ -230,8 +228,6 @@ def tile_selfattention_pa_t_kernel(tc, x, W, b, out_0, out_1, out_2):
         quantise_x(0, 0, 2)
         spread_bias(Q)
         turn_x(0, 2, "scalar")
-        spread_bias(K)
-        spread_bias(V)
         for n in range(NB):
             order = (V, Q, K) if n == NB - 1 else (Q, K, V)
             for j in range(3):
@@ -249,6 +245,9 @@ def tile_selfattention_pa_t_kernel(tc, x, W, b, out_0, out_1, out_2):
                     turn_x(n + 1, 2, "vector")
                 for t in range(BLOCK):
                     project(n, s, t)
+                    if n == 0 and j == 0 and t == 0:
+                        spread_bias(K)
+                        spread_bias(V)
                     if n + 1 < NB and (n, j, t) in ((0, 2, 2), (n, 0, 3)) and (n > 0 or j == 2):
                         quantise_x(n + 1, 0, BLOCK)
                     if s != V:

from contextlib import ExitStack

import concourse.mybir as mybir
from concourse.masks import make_identity

FP8X4 = mybir.dt.float8_e4m3fn_x4
F32 = mybir.dt.float32
BF16 = mybir.dt.bfloat16
U32 = mybir.dt.uint32
U8 = mybir.dt.uint8
ACT = mybir.ActivationFunctionType
ALU = mybir.AluOpType

B, L, E, H = 4, 1024, 512, 4
HD = E // H
Q, K, V = 0, 1, 2
P = 128
T = L // P
BLOCK = 4
NB = B * T // BLOCK
EPS = 1e-12
FLOPS = 2 * B * L * E * 3 * E
RING = 32


def tile_selfattention_pa_t_kernel(tc, x, W, b, out_0, out_1, out_2):
    nc = tc.nc
    outs = (out_0, out_1, out_2)
    with ExitStack() as ctx:
        ctx.enter_context(tc.manual_schedule())
        const = ctx.enter_context(tc.tile_pool(name="const", bufs=1))
        grp = ctx.enter_context(tc.tile_pool(name="grp", bufs=2))
        cod = ctx.enter_context(tc.tile_pool(name="cod", bufs=3))
        stg = ctx.enter_context(tc.tile_pool(name="stg", bufs=3))
        small = ctx.enter_context(tc.tile_pool(name="small", bufs=6))
        ps_t = ctx.enter_context(tc.psum_pool(name="ps_t", bufs=2))
        ps_a = ctx.enter_context(tc.psum_pool(name="ps_a", bufs=6))

        w_sb = const.tile([P, 3, H, E], BF16)
        x_sb = const.tile([P, B, T, E], BF16)
        b_rows = const.tile([P, 3 * HD], BF16)
        bias = const.tile([P, 3, H, HD], BF16)
        ident_b = const.tile([P, P], BF16)
        ident = const.tile([P, P], F32)
        c_pos = const.tile([P, 1], F32)
        c_neg = const.tile([P, 1], F32)
        warm = const.tile([P, 1], F32)
        junk = const.tile([P, RING, HD], BF16)
        w_codes = const.tile([P, 3, E], U32, align_bytes=64)
        w_scales = const.tile([P, 3, E], U8, align_bytes=64)

        def load_x(bi, t0, t1):
            nc.sync.dma_start(
                out=x_sb[:, bi].rearrange("p t k -> p (t k)")[:, t0 * E:t1 * E],
                in_=x[bi].rearrange("(p t) k -> p (t k)", t=T)[:, t0 * E:t1 * E],
            )

        def load_w(s, h0, h1):
            rows = W.rearrange("(h s p) k -> s p h k", h=H, s=3)
            nc.sync.dma_start(out=w_sb[:, s, h0:h1, :], in_=rows[s][:, h0:h1, :])

        nc.vector.memset(b_rows[:].bitcast(U32), 0)
        load_x(0, 0, 2)
        nc.sync.dma_start(out=b_rows[0:H, :], in_=b.rearrange("(h c) -> h c", h=H))
        load_w(Q, 0, 2)
        load_w(Q, 2, 4)
        load_x(0, 2, 4)
        load_w(K, 0, 4)
        load_w(V, 0, 4)
        load_x(0, 4, T)
        for bi in range(1, B):
            load_x(bi, 0, T)

        make_identity(nc, ident[:])
        make_identity(nc, ident_b[:])
        nc.vector.memset(c_pos[:], EPS * EPS)
        nc.vector.memset(c_neg[:], -EPS * EPS)
        nc.scalar.activation(out=warm[:], in_=c_pos[:], func=ACT.Abs_reciprocal_sqrt)

        def turn(tiles, pool, name, dst, engine):
            bank = pool.tile([P, 2, 2, P], F32, name=name)
            for i in range(2):
                words = tiles[i].bitcast(F32)
                for u in range(2):
                    nc.tensor.transpose(bank[:, i, u, :], words[:, u * P:(u + 1) * P], ident[:])

            def copy_out():
                src = bank[:].rearrange("p i u r -> p i r u")
                out = dst.bitcast(F32).rearrange("p (i r u) -> p i r u", i=2, u=2)
                if engine == "vector":
                    nc.vector.tensor_copy(out=out, in_=src)
                else:
                    nc.scalar.copy(out=out, in_=src)
            return copy_out

        def quantise(values, codes, scales):
            nc.vector.quantize_mx(out=codes.bitcast(FP8X4), scales=scales, in_=values)

        def turn_w(s):
            values = grp.tile([P, 4 * E], BF16, name="gw", align_bytes=64)
            copies = []
            for a, engine in ((0, "scalar"), (1, "vector")):
                tiles = [w_sb[:, s, 2 * a + i, :] for i in range(2)]
                copies.append(turn(tiles, ps_a, "acc", values[:, a * 2 * E:(a + 1) * 2 * E], engine))
            for copy_out in copies:
                copy_out()
            return values

        x_mx = {}

        def turn_x(n, t, engine):
            if n not in x_mx:
                values = grp.tile([P, BLOCK * E], BF16, name="gx", align_bytes=64)
                codes = cod.tile([P, BLOCK * P], U32, name="xc", align_bytes=64)
                scales = cod.tile([P, BLOCK * P], U8, name="xs", align_bytes=64)
                x_mx[n] = (values, codes, scales)
            first = n * BLOCK + t
            tiles = [x_sb[:, (first + i) // T, (first + i) % T, :] for i in range(2)]
            turn(tiles, ps_t, "pt", x_mx[n][0][:, t * E:(t + 2) * E], engine)()

        def quantise_x(n, t0, t1):
            values, codes, scales = x_mx[n]
            quantise(values[:, t0 * E:t1 * E], codes[:, t0 * P:t1 * P], scales[:, t0 * P:t1 * P])

        stage = {}
        sumsq = {}
        norms = {}

        def results(n, s):
            bi, t0 = n * BLOCK // T, n * BLOCK % T
            if bi not in stage:
                st_qk = stg.tile([P, 2, H, T, HD], F32, name="st_qk")
                st_v = stg.tile([P, H, T, HD], F32, name="st_v")
                stage[bi] = (st_qk, st_v)
            whole = stage[bi][1][:] if s == V else stage[bi][0][:, s]
            return whole[:, :, t0:t0 + BLOCK, :]

        def project(n, s, t):
            values, codes, scales = x_mx[n]
            cols = slice(t * P, (t + 1) * P)
            acc = ps_a.tile([P, H, HD], F32, name="acc")
            nc.tensor.matmul_mx(
                out=acc[:].rearrange("p h d -> p (h d)"),
                lhsT=codes[:, cols].bitcast(FP8X4), lhsT_scale=scales[:, cols],
                rhs=w_codes[:, s, :].bitcast(FP8X4), rhs_scale=w_scales[:, s, :],
                start=True, stop=True,
            )
            nc.vector.tensor_tensor(out=results(n, s)[:, :, t, :], in0=bias[:, s], in1=acc[:], op=ALU.add)

        def squares(n, s, t):
            if n not in sumsq:
                ss = small.tile([P, 2, H, BLOCK], F32, name="ss")
                sumsq[n] = ss
            for h in range(H):
                nc.scalar.activation(
                    out=junk[:, (s * BLOCK + t) * H + h, :], in_=results(n, s)[:, h, t, :], func=ACT.Square,
                    accum_out=sumsq[n][:, s, h, t:t + 1],
                )

        def clamp(n, s):
            if n not in norms:
                u = small.tile([P, 2, H * BLOCK], F32, name="u")
                r = small.tile([P, 2, H, BLOCK], F32, name="r")
                norms[n] = (u, r)
            nc.scalar.activation(
                out=norms[n][0][:, s], in_=sumsq[n][:, s].rearrange("p h t -> p (h t)"), func=ACT.Relu, bias=c_neg[:]
            )

        def rsqrt(n, s):
            u, r = norms[n]
            nc.scalar.activation(
                out=r[:, s].rearrange("p h t -> p (h t)"), in_=u[:, s], func=ACT.Abs_reciprocal_sqrt, bias=c_pos[:]
            )

        def scale(n, s, heads, engine):
            y, r = results(n, s), norms[n][1]
            h0, h1 = heads
            if engine == "gpsimd" and h1 > h0:
                nc.gpsimd.tensor_tensor(
                    out=y[:, h0:h1], in0=y[:, h0:h1],
                    in1=r[:, s, h0:h1].unsqueeze(3).to_broadcast([P, h1 - h0, BLOCK, HD]), op=ALU.mult,
                )
            elif engine == "scalar":
                for h in range(h0, h1):
                    for t in range(BLOCK):
                        nc.scalar.activation(out=y[:, h, t, :], in_=y[:, h, t, :], func=ACT.Copy, scale=r[:, s, h, t:t + 1])
            elif engine == "vector":
                for t in range(BLOCK):
                    for h in range(h0, h1):
                        nc.vector.tensor_scalar_mul(out=y[:, h, t, :], in0=y[:, h, t, :], scalar1=r[:, s, h, t:t + 1])

        def store(n, s):
            bi, t0 = n * BLOCK // T, n * BLOCK % T
            run = slice(t0 * HD, (t0 + BLOCK) * HD)
            whole = stage[bi][1][:] if s == V else stage[bi][0][:, s]
            nc.sync.dma_start(
                out=outs[s][bi].rearrange("h (p t) d -> p h (t d)", t=T)[:, :, run],
                in_=whole.rearrange("p h t d -> p h (t d)")[:, :, run],
            )

        def spread_bias(s):
            pb = ps_a.tile([P, H, HD], F32, name="acc")
            for h in range(H):
                nc.tensor.matmul(
                    out=pb[:, h, :], lhsT=ident_b[:, h:h + 1].to_broadcast([P, P]), rhs=b_rows[:, s * HD:(s + 1) * HD],
                    start=True, stop=True,
                )
            nc.scalar.copy(out=bias[:, s], in_=pb[:])

        waiting = []
        held = []

        def finish(n, s):
            if n == NB - 1:
                g, a = 0, s
            else:
                g, a = H - 1, H
            scale(n, s, (0, g), "gpsimd")
            scale(n, s, (g, a), "scalar")
            scale(n, s, (a, H), "vector")
            if s == Q and 0 < n < NB - 1:
                held.append((n, s))
            else:
                store(n, s)

        turn_x(0, 0, "vector")
        w_values = turn_w(Q)
        quantise_x(0, 0, 2)
        spread_bias(Q)
        turn_x(0, 2, "scalar")
        for n in range(NB):
            order = (V, Q, K) if n == NB - 1 else (Q, K, V)
            for j in range(3):
                s = order[j]
                if n == 0:
                    quantise(w_values[:], w_codes[:, s, :], w_scales[:, s, :])
                    if j == 0:
                        quantise_x(0, 2, 4)
                    else:
                        turn_x(1, 2 * j - 2, "vector")
                    if j < 2:
                        w_values = turn_w(order[j + 1])
                elif j == 0 and n + 1 < NB:
                    turn_x(n + 1, 0, "scalar" if n % 2 == 1 and n < NB - 2 else "vector")
                    turn_x(n + 1, 2, "vector")
                for t in range(BLOCK):
                    project(n, s, t)
                    if n == 0 and j == 0 and t == 0:
                        spread_bias(K)
                        spread_bias(V)
                    if n + 1 < NB and (n, j, t) in ((0, 2, 2), (n, 0, 3)) and (n > 0 or j == 2):
                        quantise_x(n + 1, 0, BLOCK)
                    if s != V:
                        squares(n, s, t)
                        if waiting and t == 0:
                            clamp(*waiting[0])
                        if waiting and t == 1:
                            rsqrt(*waiting[0])
                    elif t == BLOCK - 1:
                        store(n, V)
                        while held:
                            store(*held.pop())
                    if s != V and waiting and t == BLOCK - 1:
                        finish(*waiting.pop(0))
                if s != V:
                    waiting.append((n, s))
        clamp(*waiting[0])
        rsqrt(*waiting[0])
        finish(*waiting[0])
